import numpy as np
import ml_dtypes


def mxq(x, axis, fmt="e4m3"):
    dtype, down = {"e4m3": (ml_dtypes.float8_e4m3fn, 7), "e5m2": (ml_dtypes.float8_e5m2, 14)}[fmt]
    v = np.moveaxis(np.asarray(x, np.float32).astype(ml_dtypes.bfloat16).astype(np.float64), axis, -1)
    blocks = v.reshape(v.shape[:-1] + (-1, 32))
    amax = np.abs(blocks).max(-1, keepdims=True)
    byte = np.maximum(np.where(amax > 0, np.frexp(amax)[1] - 1 + 127, 0) - down, 1)
    scale = np.exp2(byte - 127.0)
    codes = (blocks / scale).astype(np.float32).astype(dtype).astype(np.float64)
    return np.moveaxis((codes * scale).reshape(v.shape), -1, axis)


WIDE = False


def mx_kscale(k):
    if not WIDE:
        return np.ones(k)
    levels = np.array([10, -10, 5, -5, 0])
    a = np.random.permutation(np.resize(levels, k // 512 * 4)).reshape(k // 512, 4)
    idx = np.arange(k)
    return np.exp2(a[idx // 512, idx % 128 // 32])


BF16 = ml_dtypes.bfloat16


def bf(x):
    return np.asarray(x, np.float32).astype(BF16)


def f64(x):
    return np.asarray(x).astype(np.float64)


B, N, VF_D, HID_D, EMB_D = 256, 512, 16384, 512, 512
C = 6.0 / np.sqrt(EMB_D)


def _partial_order_sim(hypers, hypos):
    act = np.maximum(hypers - hypos, 0.0)
    return -np.sqrt(np.sum(act * act, axis=-1))


def setup_inputs():
    s, t = mx_kscale(VF_D), mx_kscale(HID_D)
    return {"vfs": bf(np.random.standard_normal((B, VF_D)) * s),
            "p_lfs": bf(np.random.standard_normal((B, EMB_D)) * 2.0 * C),
            "n_lfs": bf(np.random.standard_normal((N, EMB_D)) * C),
            "W_hidden": bf(np.random.standard_normal((HID_D, VF_D)) / np.sqrt(VF_D) / s[None, :] * t[:, None]),
            "b_hidden": bf(np.random.standard_normal(HID_D) * 0.5 * t),
            "W_embed": bf(np.random.standard_normal((EMB_D, HID_D)) * C / np.sqrt(HID_D) / t[None, :]),
            "b_embed": bf(np.random.standard_normal(EMB_D) * 0.5 * C)}


def reference(vfs, p_lfs, n_lfs, W_hidden, b_hidden, W_embed, b_embed):
    vf_hidden = (mxq(f64(vfs), 1, "e4m3") @ mxq(f64(W_hidden), 1, "e4m3").T) + f64(b_hidden)
    vf_emb = (mxq(vf_hidden, 1, "e4m3") @ mxq(f64(W_embed), 1, "e4m3").T) + f64(b_embed)
    p_scores = _partial_order_sim(f64(p_lfs), vf_emb)
    n_scores = np.stack([_partial_order_sim(nl[None, :], vf_emb) for nl in f64(n_lfs)], axis=1)
    return np.concatenate([p_scores[:, None], n_scores], axis=1)

@@ -1,0 +1,369 @@
+import concourse.mybir as mybir
+from concourse.masks import make_identity
+
+F32 = mybir.dt.float32
+BF16 = mybir.dt.bfloat16
+U32 = mybir.dt.uint32
+U8 = mybir.dt.uint8
+FP8X4 = mybir.dt.float8_e4m3fn_x4
+ALU = mybir.AluOpType
+ACT = mybir.ActivationFunctionType
+
+B, N_NEG, VF_D, HID_D, EMB_D = 256, 512, 16384, 512, 512
+
+P = 128
+PACK = 4
+K_PASS = P * PACK
+PASSES = VF_D // K_PASS
+K_CHUNK = 2048
+PASSES_PER_CHUNK = K_CHUNK // K_PASS
+CHUNKS = VF_D // K_CHUNK
+B_TILES = B // P
+H_TILES = HID_D // P
+ROW_TILES = B_TILES + H_TILES
+D_CHUNKS = EMB_D // P
+J_BLOCKS = N_NEG // P
+
+FLOPS = 2 * B * VF_D * HID_D + 2 * B * HID_D * EMB_D
+
+
+def tile_hypernymvisual_acc_k_kernel(
+    tc, vfs, p_lfs, n_lfs, W_hidden, b_hidden, W_embed, b_embed, out
+):
+    nc = tc.nc
+    with tc.manual_schedule(), tc.tile_pool(name="keep", bufs=1) as keep:
+        ident_bf = keep.tile([P, P], BF16)
+        make_identity(nc, ident_bf[:])
+        ident_f32 = keep.tile([P, P], F32)
+        make_identity(nc, ident_f32[:])
+
+        one = keep.tile([P, 1], F32)
+        nc.vector.memset(one[:], 1.0)
+        one_root = keep.tile([P, 1], F32)
+        nc.scalar.activation(out=one_root[:], in_=one[:], func=ACT.Sqrt)
+
+        sums_scalar = keep.tile([P, J_BLOCKS, B], F32)
+        nc.gpsimd.memset(sums_scalar[:], 0.0)
+        sums_vector = keep.tile([P, J_BLOCKS, B], F32)
+        nc.gpsimd.memset(sums_vector[:], 0.0)
+
+        emb_t = keep.tile([P, D_CHUNKS, B], F32)
+        neg_t = keep.tile([P, D_CHUNKS, N_NEG], F32)
+        pos_t = keep.tile([P, D_CHUNKS, B], F32)
+        neg_sb = keep.tile([P, J_BLOCKS, EMB_D], BF16)
+
+        with (
+            tc.tile_pool(name="load", bufs=3) as load,
+            tc.tile_pool(name="work", bufs=3) as work,
+            tc.tile_pool(name="codes", bufs=2) as codes,
+            tc.psum_pool(name="acc_psum", bufs=1) as acc_psum,
+            tc.psum_pool(name="turn_psum", bufs=6) as turn_psum,
+        ):
+            bias_rows = keep.tile([P, P], BF16)
+            nc.vector.memset(bias_rows[:], 0.0)
+            nc.sync.dma_start(
+                out=bias_rows[0:H_TILES, :], in_=b_hidden.rearrange("(t p) -> t p", p=P)
+            )
+            nc.sync.dma_start(
+                out=bias_rows[H_TILES : H_TILES + D_CHUNKS, :],
+                in_=b_embed.rearrange("(t p) -> t p", p=P),
+            )
+            bias_ps = turn_psum.tile([P, P], BF16, tag="bank")
+            nc.tensor.transpose(out=bias_ps[:], in_=bias_rows[:], identity=ident_bf[:])
+            bias_cols = keep.tile([P, H_TILES + D_CHUNKS], F32)
+            nc.vector.tensor_copy(out=bias_cols[:], in_=bias_ps[:, 0 : H_TILES + D_CHUNKS])
+
+            we_sb = keep.tile([P, D_CHUNKS, HID_D], BF16)
+            nc.sync.dma_start(out=we_sb[:], in_=W_embed.rearrange("(c p) h -> p c h", p=P))
+            we_grouped = keep.tile([P, EMB_D, PACK], BF16, align_bytes=64)
+            for dc in range(D_CHUNKS):
+                we_ps = turn_psum.tile([P, PACK, P], BF16, tag="bank")
+                for t in range(PACK):
+                    nc.tensor.transpose(
+                        out=we_ps[:, t, :],
+                        in_=we_sb[:, dc, t * P : (t + 1) * P],
+                        identity=ident_bf[:],
+                    )
+                nc.vector.tensor_copy(
+                    out=we_grouped[:, dc * P : (dc + 1) * P, :],
+                    in_=we_ps[:].rearrange("p t r -> p r t"),
+                )
+            we_codes = keep.tile([P, EMB_D], U32, align_bytes=64)
+            we_scales = keep.tile([P, EMB_D], U8, align_bytes=64)
+            nc.vector.quantize_mx(
+                out=we_codes[:].bitcast(FP8X4),
+                scales=we_scales[:],
+                in_=we_grouped[:].rearrange("p r t -> p (r t)"),
+            )
+
+            vf_view = vfs.rearrange("(t p) k -> p t k", p=P)
+            wh_view = W_hidden.rearrange("(t p) k -> p t k", p=P)
+            acc = [acc_psum.tile([P, HID_D], F32, name="acc%d" % bt) for bt in range(B_TILES)]
+
+            def load_chunk(c):
+                rows = load.tile([P, ROW_TILES, K_CHUNK], BF16, tag="rows")
+                k_cols = slice(c * K_CHUNK, (c + 1) * K_CHUNK)
+                nc.sync.dma_start(out=rows[:, 0:B_TILES, :], in_=vf_view[:, :, k_cols])
+                nc.sync.dma_start(out=rows[:, B_TILES:ROW_TILES, :], in_=wh_view[:, :, k_cols])
+                return rows
+
+            def turn_pass(rows, gl):
+                row_words = rows[:].bitcast(F32)
+                grouped = work.tile([P, ROW_TILES * P * PACK], BF16, tag="grouped", align_bytes=64)
+                grouped_words = grouped[:].bitcast(F32).rearrange(
+                    "p (t r u) -> p t r u", t=ROW_TILES, u=2
+                )
+                for pair in range(ROW_TILES // 2):
+                    bank = turn_psum.tile([P, 2, 2, P], F32, tag="bank")
+                    for s in range(2):
+                        for u in range(2):
+                            w0 = gl * (K_PASS // 2) + u * P
+                            nc.tensor.transpose(
+                                out=bank[:, s, u, :],
+                                in_=row_words[:, 2 * pair + s, w0 : w0 + P],
+                                identity=ident_f32[:],
+                            )
+                    copy_out = nc.vector.tensor_copy if pair == 2 else nc.scalar.copy
+                    copy_out(
+                        out=grouped_words[:, 2 * pair : 2 * pair + 2, :, :],
+                        in_=bank[:].rearrange("p s u r -> p s r u"),
+                    )
+                return grouped
+
+            def new_codes():
+                vf_codes = codes.tile([P, PASSES_PER_CHUNK, B], U32, tag="vf_codes", align_bytes=64)
+                vf_scales = codes.tile([P, PASSES_PER_CHUNK, B], U8, tag="vf_scales", align_bytes=64)
+                wh_codes = codes.tile([P, PASSES_PER_CHUNK, HID_D], U32, tag="wh_codes", align_bytes=64)
+                wh_scales = codes.tile([P, PASSES_PER_CHUNK, HID_D], U8, tag="wh_scales", align_bytes=64)
+                return vf_codes, vf_scales, wh_codes, wh_scales
+
+            def quantise_pass(grouped, chunk_codes, gl):
+                vf_codes, vf_scales, wh_codes, wh_scales = chunk_codes
+                split = B * PACK
+                nc.vector.quantize_mx(
+                    out=vf_codes[:, gl, :].bitcast(FP8X4),
+                    scales=vf_scales[:, gl, :],
+                    in_=grouped[:, 0:split],
+                )
+                nc.vector.quantize_mx(
+                    out=wh_codes[:, gl, :].bitcast(FP8X4),
+                    scales=wh_scales[:, gl, :],
+                    in_=grouped[:, split:],
+                )
+
+            def multiply_chunk(c, chunk_codes):
+                vf_codes, vf_scales, wh_codes, wh_scales = chunk_codes
+                for gl in range(PASSES_PER_CHUNK):
+                    g = c * PASSES_PER_CHUNK + gl
+                    for bt in range(B_TILES):
+                        b_cols = slice(bt * P, (bt + 1) * P)
+                        nc.tensor.matmul_mx(
+                            out=acc[bt][:],
+                            lhsT=vf_codes[:, gl, b_cols].bitcast(FP8X4),
+                            lhsT_scale=vf_scales[:, gl, b_cols],
+                            rhs=wh_codes[:, gl, :].bitcast(FP8X4),
+                            rhs_scale=wh_scales[:, gl, :],
+                            start=(g == 0),
+                            stop=(g == PASSES - 1),
+                        )
+
+            waiting = None
+            last_codes = None
+            for c in range(CHUNKS):
+                rows = load_chunk(c)
+                chunk_codes = new_codes()
+                for gl in range(PASSES_PER_CHUNK):
+                    grouped = turn_pass(rows, gl)
+                    if waiting is not None:
+                        quantise_pass(*waiting)
+                    waiting = (grouped, chunk_codes, gl)
+                if c > 0:
+                    multiply_chunk(c - 1, last_codes)
+                last_codes = chunk_codes
+            quantise_pass(*waiting)
+
+            nc.sync.dma_start(out=neg_sb[:], in_=n_lfs.rearrange("(c p) d -> p c d", p=P))
+            pos_sb = keep.tile([P, B_TILES, EMB_D], BF16)
+            nc.sync.dma_start(out=pos_sb[:], in_=p_lfs.rearrange("(c p) d -> p c d", p=P))
+            for half in range(2):
+                neg_ps = turn_psum.tile([P, 2, N_NEG], BF16, tag="bank")
+                for dl in range(2):
+                    dc = 2 * half + dl
+                    for jb in range(J_BLOCKS):
+                        nc.tensor.transpose(
+                            out=neg_ps[:, dl, jb * P : (jb + 1) * P],
+                            in_=neg_sb[:, jb, dc * P : (dc + 1) * P],
+                            identity=ident_bf[:],
+                        )
+                copy_out = nc.vector.tensor_copy if half == 1 else nc.scalar.copy
+                copy_out(out=neg_t[:, 2 * half : 2 * half + 2, :], in_=neg_ps[:])
+            pos_ps = turn_psum.tile([P, D_CHUNKS, B], BF16, tag="bank")
+            for dc in range(D_CHUNKS):
+                for bt in range(B_TILES):
+                    nc.tensor.transpose(
+                        out=pos_ps[:, dc, bt * P : (bt + 1) * P],
+                        in_=pos_sb[:, bt, dc * P : (dc + 1) * P],
+                        identity=ident_bf[:],
+                    )
+            nc.scalar.copy(out=pos_t[:], in_=pos_ps[:])
+
+            multiply_chunk(CHUNKS - 1, last_codes)
+
+            hid_sb = [keep.tile([P, HID_D], F32, name="hid_sb%d" % bt) for bt in range(B_TILES)]
+            nc.scalar.copy(out=hid_sb[0][:], in_=acc[0][:])
+            nc.vector.tensor_copy(out=hid_sb[1][:], in_=acc[1][:])
+
+            def add_bias(half, out_tile, bank, first_col):
+                for l in range(2):
+                    c = 2 * half + l
+                    bias = bias_cols[:, first_col + c : first_col + c + 1]
+                    if half == 0:
+                        nc.scalar.activation(
+                            out=out_tile[:, c, :], in_=bank[:, l, :], func=ACT.Identity, bias=bias
+                        )
+                    else:
+                        nc.vector.tensor_scalar(
+                            out=out_tile[:, c, :], in0=bank[:, l, :],
+                            scalar1=bias, scalar2=None, op0=ALU.add,
+                        )
+
+            hid_bf = keep.tile([P, PACK, B], BF16)
+            for half in range(2):
+                hid_ps = turn_psum.tile([P, 2, B], F32, tag="bank")
+                for l in range(2):
+                    t = 2 * half + l
+                    for bt in range(B_TILES):
+                        nc.tensor.transpose(
+                            out=hid_ps[:, l, bt * P : (bt + 1) * P],
+                            in_=hid_sb[bt][:, t * P : (t + 1) * P],
+                            identity=ident_f32[:],
+                        )
+                add_bias(half, hid_bf, hid_ps, 0)
+            hid_grouped = keep.tile([P, B, PACK], BF16, align_bytes=64)
+            nc.vector.tensor_copy(out=hid_grouped[:], in_=hid_bf[:].rearrange("p t b -> p b t"))
+            hid_codes = keep.tile([P, B], U32, align_bytes=64)
+            hid_scales = keep.tile([P, B], U8, align_bytes=64)
+            nc.vector.quantize_mx(
+                out=hid_codes[:].bitcast(FP8X4),
+                scales=hid_scales[:],
+                in_=hid_grouped[:].rearrange("p b t -> p (b t)"),
+            )
+
+            for half in range(2):
+                emb_ps = turn_psum.tile([P, 2, B], F32, tag="bank")
+                for l in range(2):
+                    d_cols = slice((2 * half + l) * P, (2 * half + l + 1) * P)
+                    nc.tensor.matmul_mx(
+                        out=emb_ps[:, l, :],
+                        lhsT=we_codes[:, d_cols].bitcast(FP8X4),
+                        lhsT_scale=we_scales[:, d_cols],
+                        rhs=hid_codes[:].bitcast(FP8X4),
+                        rhs_scale=hid_scales[:],
+                        start=True,
+                        stop=True,
+                    )
+                add_bias(half, emb_t, emb_ps, H_TILES)
+
+        with (
+            tc.tile_pool(name="clipped", bufs=4) as clipped_pool,
+            tc.tile_pool(name="scratch", bufs=2) as scratch,
+            tc.psum_pool(name="turned_psum", bufs=6) as turned_psum,
+            tc.psum_pool(name="spread_psum", bufs=2) as spread_psum,
+        ):
+
+            def square_and_sum(clipped_cols, sum_col):
+                turned = turned_psum.tile([P, EMB_D], F32, tag="turned")
+                for dc in range(D_CHUNKS):
+                    nc.tensor.transpose(
+                        out=turned[:, dc * P : (dc + 1) * P],
+                        in_=clipped_cols(dc),
+                        identity=ident_f32[:],
+                    )
+                squares = scratch.tile([P, EMB_D], F32, tag="squares")
+                nc.scalar.activation(
+                    out=squares[:], in_=turned[:], func=ACT.Square, accum_out=sum_col
+                )
+
+            def scalar_way(i):
+                clipped = clipped_pool.tile([P, D_CHUNKS, N_NEG], F32, tag="clipped")
+                for dc in range(D_CHUNKS):
+                    nc.vector.tensor_scalar(
+                        out=clipped[:, dc, :],
+                        in0=neg_t[:, dc, :],
+                        scalar1=emb_t[:, dc, i : i + 1],
+                        scalar2=0.0,
+                        op0=ALU.subtract,
+                        op1=ALU.max,
+                    )
+                for jb in range(J_BLOCKS):
+                    square_and_sum(
+                        lambda dc: clipped[:, dc, jb * P : (jb + 1) * P],
+                        sums_scalar[:, jb, i : i + 1],
+                    )
+
+            def spread_row(i):
+                spread = spread_psum.tile([P, EMB_D], F32, tag="spread")
+                for dc in range(D_CHUNKS):
+                    nc.tensor.transpose(
+                        out=spread[:, dc * P : (dc + 1) * P],
+                        in_=emb_t[:, dc, i : i + 1].to_broadcast([P, P]),
+                        identity=ident_f32[:],
+                    )
+                return spread
+
+            def vector_way(i, jb, spread):
+                diff = scratch.tile([P, EMB_D], F32, tag="diff")
+                nc.vector.tensor_tensor(
+                    out=diff[:], in0=neg_sb[:, jb, :], in1=spread[:], op=ALU.subtract
+                )
+                products = scratch.tile([P, EMB_D], F32, tag="products")
+                nc.vector.scalar_tensor_tensor(
+                    out=products[:],
+                    in0=diff[:],
+                    scalar=0.0,
+                    in1=diff[:],
+                    op0=ALU.max,
+                    op1=ALU.mult,
+                    accum_out=sums_vector[:, jb, i : i + 1],
+                )
+
+            for first in range(0, B, J_BLOCKS + 1):
+                vector_row = first + J_BLOCKS
+                if vector_row < B:
+                    spread = spread_row(vector_row)
+                for jb in range(J_BLOCKS):
+                    if first + jb < B:
+                        scalar_way(first + jb)
+                    if vector_row < B:
+                        vector_way(vector_row, jb, spread)
+
+            pos_clipped = keep.tile([P, D_CHUNKS, B], F32)
+            nc.vector.tensor_tensor(out=pos_clipped[:], in0=pos_t[:], in1=emb_t[:], op=ALU.subtract)
+            nc.vector.tensor_scalar_max(out=pos_clipped[:], in0=pos_clipped[:], scalar1=0.0)
+            pos_sums = keep.tile([P, B_TILES], F32)
+            for bt in range(B_TILES):
+                square_and_sum(
+                    lambda dc: pos_clipped[:, dc, bt * P : (bt + 1) * P],
+                    pos_sums[:, bt : bt + 1],
+                )
+
+            for bt in range(B_TILES):
+                i_cols = slice(bt * P, (bt + 1) * P)
+                sums = scratch.tile([P, J_BLOCKS, P], F32, tag="sums")
+                nc.vector.tensor_tensor(
+                    out=sums[:], in0=sums_scalar[:, :, i_cols], in1=sums_vector[:, :, i_cols],
+                    op=ALU.add,
+                )
+                sums_ps = turned_psum.tile([P, N_NEG], F32, tag="turned")
+                for jb in range(J_BLOCKS):
+                    nc.tensor.transpose(
+                        out=sums_ps[:, jb * P : (jb + 1) * P],
+                        in_=sums[:, jb, :],
+                        identity=ident_f32[:],
+                    )
+                roots = scratch.tile([P, 1 + N_NEG], F32, tag="roots")
+                nc.scalar.activation(out=roots[:, 0:1], in_=pos_sums[:, bt : bt + 1], func=ACT.Sqrt)
+                nc.scalar.activation(out=roots[:, 1:], in_=sums_ps[:], func=ACT.Sqrt)
+                scores = scratch.tile([P, 1 + N_NEG], F32, tag="scores")
+                nc.vector.tensor_scalar_mul(out=scores[:], in0=roots[:], scalar1=-1.0)
+                nc.sync.dma_start(out=out[i_cols, :], in_=scores[:])

@@ -23,6 +23,7 @@ H_TILES = HID_D // P
 ROW_TILES = B_TILES + H_TILES
 D_CHUNKS = EMB_D // P
 J_BLOCKS = N_NEG // P
+CLOCK_PASSES = 2
 
 FLOPS = 2 * B * VF_D * HID_D + 2 * B * HID_D * EMB_D
 
@@ -267,9 +268,23 @@ def tile_hypernymvisual_acc_k_kernel(
         with (
             tc.tile_pool(name="clipped", bufs=4) as clipped_pool,
             tc.tile_pool(name="scratch", bufs=2) as scratch,
-            tc.psum_pool(name="turned_psum", bufs=6) as turned_psum,
+            tc.psum_pool(name="turned_psum", bufs=5) as turned_psum,
             tc.psum_pool(name="spread_psum", bufs=2) as spread_psum,
+            tc.psum_pool(name="idle_psum", bufs=1) as idle_psum,
         ):
+            unread = idle_psum.tile([P, EMB_D], F32)
+
+            def keep_clock_up():
+                for repeat in range(CLOCK_PASSES):
+                    nc.tensor.matmul_mx(
+                        out=unread[:],
+                        lhsT=we_codes[:, 0:P].bitcast(FP8X4),
+                        lhsT_scale=we_scales[:, 0:P],
+                        rhs=we_codes[:].bitcast(FP8X4),
+                        rhs_scale=we_scales[:],
+                        start=True,
+                        stop=True,
+                    )
 
             def square_and_sum(clipped_cols, sum_col):
                 turned = turned_psum.tile([P, EMB_D], F32, tag="turned")
@@ -300,6 +315,7 @@ def tile_hypernymvisual_acc_k_kernel(
                         lambda dc: clipped[:, dc, jb * P : (jb + 1) * P],
                         sums_scalar[:, jb, i : i + 1],
                     )
+                keep_clock_up()
 
             def spread_row(i):
                 spread = spread_psum.tile([P, EMB_D], F32, tag="spread")

@@ -327,11 +327,14 @@ def tile_hypernymvisual_acc_k_kernel(
                     )
                 return spread
 
-            def vector_way(i, jb, spread):
+            def vector_way_subtract(jb, spread):
                 diff = scratch.tile([P, EMB_D], F32, tag="diff")
                 nc.vector.tensor_tensor(
                     out=diff[:], in0=neg_sb[:, jb, :], in1=spread[:], op=ALU.subtract
                 )
+                return diff
+
+            def vector_way_square_and_sum(i, jb, diff):
                 products = scratch.tile([P, EMB_D], F32, tag="products")
                 nc.vector.scalar_tensor_tensor(
                     out=products[:],
@@ -348,10 +351,12 @@ def tile_hypernymvisual_acc_k_kernel(
                 if vector_row < B:
                     spread = spread_row(vector_row)
                 for jb in range(J_BLOCKS):
+                    if vector_row < B:
+                        diff = vector_way_subtract(jb, spread)
                     if first + jb < B:
                         scalar_way(first + jb)
                     if vector_row < B:
-                        vector_way(vector_row, jb, spread)
+                        vector_way_square_and_sum(vector_row, jb, diff)
 
             pos_clipped = keep.tile([P, D_CHUNKS, B], F32)
             nc.vector.tensor_tensor(out=pos_clipped[:], in0=pos_t[:], in1=emb_t[:], op=ALU.subtract)

@@ -23,7 +23,9 @@ H_TILES = HID_D // P
 ROW_TILES = B_TILES + H_TILES
 D_CHUNKS = EMB_D // P
 J_BLOCKS = N_NEG // P
-CLOCK_PASSES = 2
+VECTOR_BLOCK = 0
+STATS = 6
+CLOCK_PASSES = 1
 
 FLOPS = 2 * B * VF_D * HID_D + 2 * B * HID_D * EMB_D
 
@@ -43,10 +45,7 @@ def tile_hypernymvisual_acc_k_kernel(
         one_root = keep.tile([P, 1], F32)
         nc.scalar.activation(out=one_root[:], in_=one[:], func=ACT.Sqrt)
 
-        sums_scalar = keep.tile([P, J_BLOCKS, B], F32)
-        nc.gpsimd.memset(sums_scalar[:], 0.0)
-        sums_vector = keep.tile([P, J_BLOCKS, B], F32)
-        nc.gpsimd.memset(sums_vector[:], 0.0)
+        sums = keep.tile([P, J_BLOCKS, B], F32)
 
         emb_t = keep.tile([P, D_CHUNKS, B], F32)
         neg_t = keep.tile([P, D_CHUNKS, N_NEG], F32)
@@ -268,11 +267,11 @@ def tile_hypernymvisual_acc_k_kernel(
         with (
             tc.tile_pool(name="clipped", bufs=4) as clipped_pool,
             tc.tile_pool(name="scratch", bufs=2) as scratch,
-            tc.psum_pool(name="turned_psum", bufs=5) as turned_psum,
-            tc.psum_pool(name="spread_psum", bufs=2) as spread_psum,
-            tc.psum_pool(name="idle_psum", bufs=1) as idle_psum,
+            tc.psum_pool(name="scalar_psum", bufs=5) as scalar_psum,
+            tc.psum_pool(name="vector_psum", bufs=2) as vector_psum,
+            tc.psum_pool(name="unread_psum", bufs=1) as unread_psum,
         ):
-            unread = idle_psum.tile([P, EMB_D], F32)
+            unread = unread_psum.tile([P, EMB_D], F32)
 
             def keep_clock_up():
                 for repeat in range(CLOCK_PASSES):
@@ -286,20 +285,23 @@ def tile_hypernymvisual_acc_k_kernel(
                         stop=True,
                     )
 
-            def square_and_sum(clipped_cols, sum_col):
-                turned = turned_psum.tile([P, EMB_D], F32, tag="turned")
+            def turn(pool, clipped, x_cols):
+                turned = pool.tile([P, EMB_D], F32, tag="turned")
                 for dc in range(D_CHUNKS):
                     nc.tensor.transpose(
                         out=turned[:, dc * P : (dc + 1) * P],
-                        in_=clipped_cols(dc),
+                        in_=clipped[:, dc, x_cols],
                         identity=ident_f32[:],
                     )
+                return turned
+
+            def scalar_sum_of_squares(turned, sum_col):
                 squares = scratch.tile([P, EMB_D], F32, tag="squares")
                 nc.scalar.activation(
                     out=squares[:], in_=turned[:], func=ACT.Square, accum_out=sum_col
                 )
 
-            def scalar_way(i):
+            def clip_and_turn(i):
                 clipped = clipped_pool.tile([P, D_CHUNKS, N_NEG], F32, tag="clipped")
                 for dc in range(D_CHUNKS):
                     nc.vector.tensor_scalar(
@@ -310,78 +312,59 @@ def tile_hypernymvisual_acc_k_kernel(
                         op0=ALU.subtract,
                         op1=ALU.max,
                     )
+                vector_bank = None
                 for jb in range(J_BLOCKS):
-                    square_and_sum(
-                        lambda dc: clipped[:, dc, jb * P : (jb + 1) * P],
-                        sums_scalar[:, jb, i : i + 1],
-                    )
+                    j_cols = slice(jb * P, (jb + 1) * P)
+                    if jb == VECTOR_BLOCK:
+                        vector_bank = turn(vector_psum, clipped, j_cols)
+                    else:
+                        scalar_sum_of_squares(
+                            turn(scalar_psum, clipped, j_cols), sums[:, jb, i : i + 1]
+                        )
                 keep_clock_up()
+                return vector_bank
 
-            def spread_row(i):
-                spread = spread_psum.tile([P, EMB_D], F32, tag="spread")
-                for dc in range(D_CHUNKS):
-                    nc.tensor.transpose(
-                        out=spread[:, dc * P : (dc + 1) * P],
-                        in_=emb_t[:, dc, i : i + 1].to_broadcast([P, P]),
-                        identity=ident_f32[:],
-                    )
-                return spread
+            stats = keep.tile([P, B, STATS], F32)
+            bank_before = None
+            for i in range(B):
+                vector_bank = clip_and_turn(i)
+                if bank_before is not None:
+                    nc.vector.bn_stats(out=stats[:, i - 1, :], in_=bank_before[:])
+                bank_before = vector_bank
+            nc.vector.bn_stats(out=stats[:, B - 1, :], in_=bank_before[:])
 
-            def vector_way_subtract(jb, spread):
-                diff = scratch.tile([P, EMB_D], F32, tag="diff")
-                nc.vector.tensor_tensor(
-                    out=diff[:], in0=neg_sb[:, jb, :], in1=spread[:], op=ALU.subtract
-                )
-                return diff
-
-            def vector_way_square_and_sum(i, jb, diff):
-                products = scratch.tile([P, EMB_D], F32, tag="products")
-                nc.vector.scalar_tensor_tensor(
-                    out=products[:],
-                    in0=diff[:],
-                    scalar=0.0,
-                    in1=diff[:],
-                    op0=ALU.max,
-                    op1=ALU.mult,
-                    accum_out=sums_vector[:, jb, i : i + 1],
-                )
-
-            for first in range(0, B, J_BLOCKS + 1):
-                vector_row = first + J_BLOCKS
-                if vector_row < B:
-                    spread = spread_row(vector_row)
-                for jb in range(J_BLOCKS):
-                    if vector_row < B:
-                        diff = vector_way_subtract(jb, spread)
-                    if first + jb < B:
-                        scalar_way(first + jb)
-                    if vector_row < B:
-                        vector_way_square_and_sum(vector_row, jb, diff)
+            halves = stats[:].rearrange("p i (h k) -> p i h k", k=STATS // 2)
+            mean_squares = keep.tile([P, B, 2], F32)
+            nc.vector.tensor_tensor(
+                out=mean_squares[:], in0=halves[:, :, :, 1], in1=halves[:, :, :, 1], op=ALU.mult
+            )
+            half_sums = keep.tile([P, B, 2], F32)
+            nc.vector.scalar_tensor_tensor(
+                out=half_sums[:],
+                in0=mean_squares[:],
+                scalar=float(EMB_D // 2),
+                in1=halves[:, :, :, 2],
+                op0=ALU.mult,
+                op1=ALU.add,
+            )
+            nc.vector.tensor_tensor(
+                out=sums[:, VECTOR_BLOCK, :], in0=half_sums[:, :, 0], in1=half_sums[:, :, 1],
+                op=ALU.add,
+            )
 
             pos_clipped = keep.tile([P, D_CHUNKS, B], F32)
             nc.vector.tensor_tensor(out=pos_clipped[:], in0=pos_t[:], in1=emb_t[:], op=ALU.subtract)
             nc.vector.tensor_scalar_max(out=pos_clipped[:], in0=pos_clipped[:], scalar1=0.0)
             pos_sums = keep.tile([P, B_TILES], F32)
             for bt in range(B_TILES):
-                square_and_sum(
-                    lambda dc: pos_clipped[:, dc, bt * P : (bt + 1) * P],
+                scalar_sum_of_squares(
+                    turn(scalar_psum, pos_clipped, slice(bt * P, (bt + 1) * P)),
                     pos_sums[:, bt : bt + 1],
                 )
 
             for bt in range(B_TILES):
                 i_cols = slice(bt * P, (bt + 1) * P)
-                sums = scratch.tile([P, J_BLOCKS, P], F32, tag="sums")
-                nc.vector.tensor_tensor(
-                    out=sums[:], in0=sums_scalar[:, :, i_cols], in1=sums_vector[:, :, i_cols],
-                    op=ALU.add,
-                )
-                sums_ps = turned_psum.tile([P, N_NEG], F32, tag="turned")
-                for jb in range(J_BLOCKS):
-                    nc.tensor.transpose(
-                        out=sums_ps[:, jb * P : (jb + 1) * P],
-                        in_=sums[:, jb, :],
-                        identity=ident_f32[:],
-                    )
+                sums_ps = turn(scalar_psum, sums, i_cols)
                 roots = scratch.tile([P, 1 + N_NEG], F32, tag="roots")
                 nc.scalar.activation(out=roots[:, 0:1], in_=pos_sums[:, bt : bt + 1], func=ACT.Sqrt)
                 nc.scalar.activation(out=roots[:, 1:], in_=sums_ps[:], func=ACT.Sqrt)

@@ -12,20 +12,20 @@ ACT = mybir.ActivationFunctionType
 B, N_NEG, VF_D, HID_D, EMB_D = 256, 512, 16384, 512, 512
 
 P = 128
-PACK = 4
-K_PASS = P * PACK
-PASSES = VF_D // K_PASS
+QUAD = 4
+K_PASS = P * QUAD
 K_CHUNK = 2048
 PASSES_PER_CHUNK = K_CHUNK // K_PASS
 CHUNKS = VF_D // K_CHUNK
 B_TILES = B // P
 H_TILES = HID_D // P
 ROW_TILES = B_TILES + H_TILES
-D_CHUNKS = EMB_D // P
-J_BLOCKS = N_NEG // P
-VECTOR_BLOCK = 0
+D_TILES = EMB_D // P
+J_TILES = N_NEG // P
+VECTOR_J_TILE = 0
 STATS = 6
-CLOCK_PASSES = 1
+PSUM_BANKS = 8
+PER_BANK = 4
 
 FLOPS = 2 * B * VF_D * HID_D + 2 * B * HID_D * EMB_D
 
@@ -45,19 +45,16 @@ def tile_hypernymvisual_acc_k_kernel(
         one_root = keep.tile([P, 1], F32)
         nc.scalar.activation(out=one_root[:], in_=one[:], func=ACT.Sqrt)
 
-        sums = keep.tile([P, J_BLOCKS, B], F32)
-
-        emb_t = keep.tile([P, D_CHUNKS, B], F32)
-        neg_t = keep.tile([P, D_CHUNKS, N_NEG], F32)
-        pos_t = keep.tile([P, D_CHUNKS, B], F32)
-        neg_sb = keep.tile([P, J_BLOCKS, EMB_D], BF16)
+        emb_t = keep.tile([P, D_TILES, B], F32)
+        neg_t = keep.tile([P, D_TILES, N_NEG], F32)
+        pos_t = keep.tile([P, D_TILES, B], F32)
 
         with (
             tc.tile_pool(name="load", bufs=3) as load,
             tc.tile_pool(name="work", bufs=3) as work,
             tc.tile_pool(name="codes", bufs=2) as codes,
             tc.psum_pool(name="acc_psum", bufs=1) as acc_psum,
-            tc.psum_pool(name="turn_psum", bufs=6) as turn_psum,
+            tc.psum_pool(name="bank_psum", bufs=PSUM_BANKS - B_TILES) as bank_psum,
         ):
             bias_rows = keep.tile([P, P], BF16)
             nc.vector.memset(bias_rows[:], 0.0)
@@ -65,27 +62,27 @@ def tile_hypernymvisual_acc_k_kernel(
                 out=bias_rows[0:H_TILES, :], in_=b_hidden.rearrange("(t p) -> t p", p=P)
             )
             nc.sync.dma_start(
-                out=bias_rows[H_TILES : H_TILES + D_CHUNKS, :],
+                out=bias_rows[H_TILES : H_TILES + D_TILES, :],
                 in_=b_embed.rearrange("(t p) -> t p", p=P),
             )
-            bias_ps = turn_psum.tile([P, P], BF16, tag="bank")
+            bias_ps = bank_psum.tile([P, P], BF16, tag="bank")
             nc.tensor.transpose(out=bias_ps[:], in_=bias_rows[:], identity=ident_bf[:])
-            bias_cols = keep.tile([P, H_TILES + D_CHUNKS], F32)
-            nc.vector.tensor_copy(out=bias_cols[:], in_=bias_ps[:, 0 : H_TILES + D_CHUNKS])
+            bias_cols = keep.tile([P, H_TILES + D_TILES], F32)
+            nc.vector.tensor_copy(out=bias_cols[:], in_=bias_ps[:, 0 : H_TILES + D_TILES])
 
-            we_sb = keep.tile([P, D_CHUNKS, HID_D], BF16)
-            nc.sync.dma_start(out=we_sb[:], in_=W_embed.rearrange("(c p) h -> p c h", p=P))
-            we_grouped = keep.tile([P, EMB_D, PACK], BF16, align_bytes=64)
-            for dc in range(D_CHUNKS):
-                we_ps = turn_psum.tile([P, PACK, P], BF16, tag="bank")
-                for t in range(PACK):
+            we_sb = keep.tile([P, D_TILES, HID_D], BF16)
+            nc.sync.dma_start(out=we_sb[:], in_=W_embed.rearrange("(dt p) h -> p dt h", p=P))
+            we_grouped = keep.tile([P, EMB_D, QUAD], BF16, align_bytes=64)
+            for dt in range(D_TILES):
+                we_ps = bank_psum.tile([P, QUAD, P], BF16, tag="bank")
+                for t in range(QUAD):
                     nc.tensor.transpose(
                         out=we_ps[:, t, :],
-                        in_=we_sb[:, dc, t * P : (t + 1) * P],
+                        in_=we_sb[:, dt, t * P : (t + 1) * P],
                         identity=ident_bf[:],
                     )
                 nc.vector.tensor_copy(
-                    out=we_grouped[:, dc * P : (dc + 1) * P, :],
+                    out=we_grouped[:, dt * P : (dt + 1) * P, :],
                     in_=we_ps[:].rearrange("p t r -> p r t"),
                 )
             we_codes = keep.tile([P, EMB_D], U32, align_bytes=64)
@@ -107,25 +104,25 @@ def tile_hypernymvisual_acc_k_kernel(
                 nc.sync.dma_start(out=rows[:, B_TILES:ROW_TILES, :], in_=wh_view[:, :, k_cols])
                 return rows
 
-            def turn_pass(rows, gl):
-                row_words = rows[:].bitcast(F32)
-                grouped = work.tile([P, ROW_TILES * P * PACK], BF16, tag="grouped", align_bytes=64)
-                grouped_words = grouped[:].bitcast(F32).rearrange(
+            def transpose_pass(rows, g):
+                rows_f32 = rows[:].bitcast(F32)
+                grouped = work.tile([P, ROW_TILES * P * QUAD], BF16, tag="grouped", align_bytes=64)
+                grouped_f32 = grouped[:].bitcast(F32).rearrange(
                     "p (t r u) -> p t r u", t=ROW_TILES, u=2
                 )
-                for pair in range(ROW_TILES // 2):
-                    bank = turn_psum.tile([P, 2, 2, P], F32, tag="bank")
+                for first_tile in range(0, ROW_TILES, 2):
+                    bank = bank_psum.tile([P, 2, 2, P], F32, tag="bank")
                     for s in range(2):
                         for u in range(2):
-                            w0 = gl * (K_PASS // 2) + u * P
+                            col = g * (K_PASS // 2) + u * P
                             nc.tensor.transpose(
                                 out=bank[:, s, u, :],
-                                in_=row_words[:, 2 * pair + s, w0 : w0 + P],
+                                in_=rows_f32[:, first_tile + s, col : col + P],
                                 identity=ident_f32[:],
                             )
-                    copy_out = nc.vector.tensor_copy if pair == 2 else nc.scalar.copy
+                    copy_out = nc.scalar.copy if first_tile + 2 < ROW_TILES else nc.vector.tensor_copy
                     copy_out(
-                        out=grouped_words[:, 2 * pair : 2 * pair + 2, :, :],
+                        out=grouped_f32[:, first_tile : first_tile + 2, :, :],
                         in_=bank[:].rearrange("p s u r -> p s r u"),
                     )
                 return grouped
@@ -137,109 +134,109 @@ def tile_hypernymvisual_acc_k_kernel(
                 wh_scales = codes.tile([P, PASSES_PER_CHUNK, HID_D], U8, tag="wh_scales", align_bytes=64)
                 return vf_codes, vf_scales, wh_codes, wh_scales
 
-            def quantise_pass(grouped, chunk_codes, gl):
+            def quantise_pass(grouped, chunk_codes, g):
                 vf_codes, vf_scales, wh_codes, wh_scales = chunk_codes
-                split = B * PACK
+                vf_end = B * QUAD
                 nc.vector.quantize_mx(
-                    out=vf_codes[:, gl, :].bitcast(FP8X4),
-                    scales=vf_scales[:, gl, :],
-                    in_=grouped[:, 0:split],
+                    out=vf_codes[:, g, :].bitcast(FP8X4),
+                    scales=vf_scales[:, g, :],
+                    in_=grouped[:, 0:vf_end],
                 )
                 nc.vector.quantize_mx(
-                    out=wh_codes[:, gl, :].bitcast(FP8X4),
-                    scales=wh_scales[:, gl, :],
-                    in_=grouped[:, split:],
+                    out=wh_codes[:, g, :].bitcast(FP8X4),
+                    scales=wh_scales[:, g, :],
+                    in_=grouped[:, vf_end:],
                 )
 
             def multiply_chunk(c, chunk_codes):
                 vf_codes, vf_scales, wh_codes, wh_scales = chunk_codes
-                for gl in range(PASSES_PER_CHUNK):
-                    g = c * PASSES_PER_CHUNK + gl
+                for g in range(PASSES_PER_CHUNK):
                     for bt in range(B_TILES):
                         b_cols = slice(bt * P, (bt + 1) * P)
                         nc.tensor.matmul_mx(
                             out=acc[bt][:],
-                            lhsT=vf_codes[:, gl, b_cols].bitcast(FP8X4),
-                            lhsT_scale=vf_scales[:, gl, b_cols],
-                            rhs=wh_codes[:, gl, :].bitcast(FP8X4),
-                            rhs_scale=wh_scales[:, gl, :],
-                            start=(g == 0),
-                            stop=(g == PASSES - 1),
+                            lhsT=vf_codes[:, g, b_cols].bitcast(FP8X4),
+                            lhsT_scale=vf_scales[:, g, b_cols],
+                            rhs=wh_codes[:, g, :].bitcast(FP8X4),
+                            rhs_scale=wh_scales[:, g, :],
+                            start=(c == 0 and g == 0),
+                            stop=(c == CHUNKS - 1 and g == PASSES_PER_CHUNK - 1),
                         )
 
             waiting = None
-            last_codes = None
+            codes_before = None
             for c in range(CHUNKS):
                 rows = load_chunk(c)
                 chunk_codes = new_codes()
-                for gl in range(PASSES_PER_CHUNK):
-                    grouped = turn_pass(rows, gl)
+                for g in range(PASSES_PER_CHUNK):
+                    grouped = transpose_pass(rows, g)
                     if waiting is not None:
                         quantise_pass(*waiting)
-                    waiting = (grouped, chunk_codes, gl)
+                    waiting = (grouped, chunk_codes, g)
                 if c > 0:
-                    multiply_chunk(c - 1, last_codes)
-                last_codes = chunk_codes
+                    multiply_chunk(c - 1, codes_before)
+                codes_before = chunk_codes
             quantise_pass(*waiting)
 
-            nc.sync.dma_start(out=neg_sb[:], in_=n_lfs.rearrange("(c p) d -> p c d", p=P))
+            neg_sb = keep.tile([P, J_TILES, EMB_D], BF16)
+            nc.sync.dma_start(out=neg_sb[:], in_=n_lfs.rearrange("(jt p) d -> p jt d", p=P))
             pos_sb = keep.tile([P, B_TILES, EMB_D], BF16)
-            nc.sync.dma_start(out=pos_sb[:], in_=p_lfs.rearrange("(c p) d -> p c d", p=P))
-            for half in range(2):
-                neg_ps = turn_psum.tile([P, 2, N_NEG], BF16, tag="bank")
-                for dl in range(2):
-                    dc = 2 * half + dl
-                    for jb in range(J_BLOCKS):
+            nc.sync.dma_start(out=pos_sb[:], in_=p_lfs.rearrange("(bt p) d -> p bt d", p=P))
+            for first_dt in range(0, D_TILES, 2):
+                neg_ps = bank_psum.tile([P, 2, N_NEG], BF16, tag="bank")
+                for s in range(2):
+                    d_cols = slice((first_dt + s) * P, (first_dt + s + 1) * P)
+                    for jt in range(J_TILES):
                         nc.tensor.transpose(
-                            out=neg_ps[:, dl, jb * P : (jb + 1) * P],
-                            in_=neg_sb[:, jb, dc * P : (dc + 1) * P],
+                            out=neg_ps[:, s, jt * P : (jt + 1) * P],
+                            in_=neg_sb[:, jt, d_cols],
                             identity=ident_bf[:],
                         )
-                copy_out = nc.vector.tensor_copy if half == 1 else nc.scalar.copy
-                copy_out(out=neg_t[:, 2 * half : 2 * half + 2, :], in_=neg_ps[:])
-            pos_ps = turn_psum.tile([P, D_CHUNKS, B], BF16, tag="bank")
-            for dc in range(D_CHUNKS):
+                copy_out = nc.scalar.copy if first_dt == 0 else nc.vector.tensor_copy
+                copy_out(out=neg_t[:, first_dt : first_dt + 2, :], in_=neg_ps[:])
+            pos_ps = bank_psum.tile([P, D_TILES, B], BF16, tag="bank")
+            for dt in range(D_TILES):
                 for bt in range(B_TILES):
                     nc.tensor.transpose(
-                        out=pos_ps[:, dc, bt * P : (bt + 1) * P],
-                        in_=pos_sb[:, bt, dc * P : (dc + 1) * P],
+                        out=pos_ps[:, dt, bt * P : (bt + 1) * P],
+                        in_=pos_sb[:, bt, dt * P : (dt + 1) * P],
                         identity=ident_bf[:],
                     )
             nc.scalar.copy(out=pos_t[:], in_=pos_ps[:])
 
-            multiply_chunk(CHUNKS - 1, last_codes)
+            multiply_chunk(CHUNKS - 1, codes_before)
 
             hid_sb = [keep.tile([P, HID_D], F32, name="hid_sb%d" % bt) for bt in range(B_TILES)]
             nc.scalar.copy(out=hid_sb[0][:], in_=acc[0][:])
             nc.vector.tensor_copy(out=hid_sb[1][:], in_=acc[1][:])
 
-            def add_bias(half, out_tile, bank, first_col):
-                for l in range(2):
-                    c = 2 * half + l
-                    bias = bias_cols[:, first_col + c : first_col + c + 1]
-                    if half == 0:
+            def add_bias(first_t, out_tile, bank, bias_col):
+                for s in range(2):
+                    t = first_t + s
+                    bias = bias_cols[:, bias_col + t : bias_col + t + 1]
+                    if first_t == 0:
                         nc.scalar.activation(
-                            out=out_tile[:, c, :], in_=bank[:, l, :], func=ACT.Identity, bias=bias
+                            out=out_tile[:, t, :], in_=bank[:, s, :], func=ACT.Identity, bias=bias
                         )
                     else:
                         nc.vector.tensor_scalar(
-                            out=out_tile[:, c, :], in0=bank[:, l, :],
+                            out=out_tile[:, t, :], in0=bank[:, s, :],
                             scalar1=bias, scalar2=None, op0=ALU.add,
                         )
 
-            hid_bf = keep.tile([P, PACK, B], BF16)
-            for half in range(2):
-                hid_ps = turn_psum.tile([P, 2, B], F32, tag="bank")
-                for l in range(2):
-                    t = 2 * half + l
+            hid_bf = keep.tile([P, H_TILES, B], BF16)
+            for first_t in range(0, H_TILES, 2):
+                hid_ps = bank_psum.tile([P, 2, B], F32, tag="bank")
+                for s in range(2):
+                    h_cols = slice((first_t + s) * P, (first_t + s + 1) * P)
                     for bt in range(B_TILES):
                         nc.tensor.transpose(
-                            out=hid_ps[:, l, bt * P : (bt + 1) * P],
-                            in_=hid_sb[bt][:, t * P : (t + 1) * P],
+                            out=hid_ps[:, s, bt * P : (bt + 1) * P],
+                            in_=hid_sb[bt][:, h_cols],
                             identity=ident_f32[:],
                         )
-                add_bias(half, hid_bf, hid_ps, 0)
-            hid_grouped = keep.tile([P, B, PACK], BF16, align_bytes=64)
+                add_bias(first_t, hid_bf, hid_ps, 0)
+            hid_grouped = keep.tile([P, B, QUAD], BF16, align_bytes=64)
             nc.vector.tensor_copy(out=hid_grouped[:], in_=hid_bf[:].rearrange("p t b -> p b t"))
             hid_codes = keep.tile([P, B], U32, align_bytes=64)
             hid_scales = keep.tile([P, B], U8, align_bytes=64)
@@ -249,12 +246,12 @@ def tile_hypernymvisual_acc_k_kernel(
                 in_=hid_grouped[:].rearrange("p b t -> p (b t)"),
             )
 
-            for half in range(2):
-                emb_ps = turn_psum.tile([P, 2, B], F32, tag="bank")
-                for l in range(2):
-                    d_cols = slice((2 * half + l) * P, (2 * half + l + 1) * P)
+            for first_dt in range(0, D_TILES, 2):
+                emb_ps = bank_psum.tile([P, 2, B], F32, tag="bank")
+                for s in range(2):
+                    d_cols = slice((first_dt + s) * P, (first_dt + s + 1) * P)
                     nc.tensor.matmul_mx(
-                        out=emb_ps[:, l, :],
+                        out=emb_ps[:, s, :],
                         lhsT=we_codes[:, d_cols].bitcast(FP8X4),
                         lhsT_scale=we_scales[:, d_cols],
                         rhs=hid_codes[:].bitcast(FP8X4),
@@ -262,72 +259,57 @@ def tile_hypernymvisual_acc_k_kernel(
                         start=True,
                         stop=True,
                     )
-                add_bias(half, emb_t, emb_ps, H_TILES)
+                add_bias(first_dt, emb_t, emb_ps, H_TILES)
 
         with (
             tc.tile_pool(name="clipped", bufs=4) as clipped_pool,
             tc.tile_pool(name="scratch", bufs=2) as scratch,
-            tc.psum_pool(name="scalar_psum", bufs=5) as scalar_psum,
             tc.psum_pool(name="vector_psum", bufs=2) as vector_psum,
-            tc.psum_pool(name="unread_psum", bufs=1) as unread_psum,
+            tc.psum_pool(name="scalar_psum", bufs=PSUM_BANKS - 2) as scalar_psum,
         ):
-            unread = unread_psum.tile([P, EMB_D], F32)
 
-            def keep_clock_up():
-                for repeat in range(CLOCK_PASSES):
-                    nc.tensor.matmul_mx(
-                        out=unread[:],
-                        lhsT=we_codes[:, 0:P].bitcast(FP8X4),
-                        lhsT_scale=we_scales[:, 0:P],
-                        rhs=we_codes[:].bitcast(FP8X4),
-                        rhs_scale=we_scales[:],
-                        start=True,
-                        stop=True,
-                    )
-
-            def turn(pool, clipped, x_cols):
-                turned = pool.tile([P, EMB_D], F32, tag="turned")
-                for dc in range(D_CHUNKS):
+            def transpose_four(pool, source, cols):
+                bank = pool.tile([P, PER_BANK * P], F32, tag="bank")
+                for t in range(PER_BANK):
                     nc.tensor.transpose(
-                        out=turned[:, dc * P : (dc + 1) * P],
-                        in_=clipped[:, dc, x_cols],
+                        out=bank[:, t * P : (t + 1) * P],
+                        in_=source[:, t, cols],
                         identity=ident_f32[:],
                     )
-                return turned
+                return bank
 
-            def scalar_sum_of_squares(turned, sum_col):
+            def scalar_sum_of_squares(bank, sum_col):
                 squares = scratch.tile([P, EMB_D], F32, tag="squares")
-                nc.scalar.activation(
-                    out=squares[:], in_=turned[:], func=ACT.Square, accum_out=sum_col
-                )
+                nc.scalar.activation(out=squares[:], in_=bank[:], func=ACT.Square, accum_out=sum_col)
 
-            def clip_and_turn(i):
-                clipped = clipped_pool.tile([P, D_CHUNKS, N_NEG], F32, tag="clipped")
-                for dc in range(D_CHUNKS):
+            sums = keep.tile([P, J_TILES, B], F32)
+
+            def clip_and_transpose(i):
+                clipped = clipped_pool.tile([P, D_TILES, N_NEG], F32, tag="clipped")
+                for dt in range(D_TILES):
                     nc.vector.tensor_scalar(
-                        out=clipped[:, dc, :],
-                        in0=neg_t[:, dc, :],
-                        scalar1=emb_t[:, dc, i : i + 1],
+                        out=clipped[:, dt, :],
+                        in0=neg_t[:, dt, :],
+                        scalar1=emb_t[:, dt, i : i + 1],
                         scalar2=0.0,
                         op0=ALU.subtract,
                         op1=ALU.max,
                     )
                 vector_bank = None
-                for jb in range(J_BLOCKS):
-                    j_cols = slice(jb * P, (jb + 1) * P)
-                    if jb == VECTOR_BLOCK:
-                        vector_bank = turn(vector_psum, clipped, j_cols)
+                for jt in range(J_TILES):
+                    j_cols = slice(jt * P, (jt + 1) * P)
+                    if jt == VECTOR_J_TILE:
+                        vector_bank = transpose_four(vector_psum, clipped, j_cols)
                     else:
                         scalar_sum_of_squares(
-                            turn(scalar_psum, clipped, j_cols), sums[:, jb, i : i + 1]
+                            transpose_four(scalar_psum, clipped, j_cols), sums[:, jt, i : i + 1]
                         )
-                keep_clock_up()
                 return vector_bank
 
             stats = keep.tile([P, B, STATS], F32)
             bank_before = None
             for i in range(B):
-                vector_bank = clip_and_turn(i)
+                vector_bank = clip_and_transpose(i)
                 if bank_before is not None:
                     nc.vector.bn_stats(out=stats[:, i - 1, :], in_=bank_before[:])
                 bank_before = vector_bank
@@ -348,23 +330,23 @@ def tile_hypernymvisual_acc_k_kernel(
                 op1=ALU.add,
             )
             nc.vector.tensor_tensor(
-                out=sums[:, VECTOR_BLOCK, :], in0=half_sums[:, :, 0], in1=half_sums[:, :, 1],
+                out=sums[:, VECTOR_J_TILE, :], in0=half_sums[:, :, 0], in1=half_sums[:, :, 1],
                 op=ALU.add,
             )
 
-            pos_clipped = keep.tile([P, D_CHUNKS, B], F32)
+            pos_clipped = keep.tile([P, D_TILES, B], F32)
             nc.vector.tensor_tensor(out=pos_clipped[:], in0=pos_t[:], in1=emb_t[:], op=ALU.subtract)
             nc.vector.tensor_scalar_max(out=pos_clipped[:], in0=pos_clipped[:], scalar1=0.0)
             pos_sums = keep.tile([P, B_TILES], F32)
             for bt in range(B_TILES):
                 scalar_sum_of_squares(
-                    turn(scalar_psum, pos_clipped, slice(bt * P, (bt + 1) * P)),
+                    transpose_four(scalar_psum, pos_clipped, slice(bt * P, (bt + 1) * P)),
                     pos_sums[:, bt : bt + 1],
                 )
 
             for bt in range(B_TILES):
                 i_cols = slice(bt * P, (bt + 1) * P)
-                sums_ps = turn(scalar_psum, sums, i_cols)
+                sums_ps = transpose_four(scalar_psum, sums, i_cols)
                 roots = scratch.tile([P, 1 + N_NEG], F32, tag="roots")
                 nc.scalar.activation(out=roots[:, 0:1], in_=pos_sums[:, bt : bt + 1], func=ACT.Sqrt)
                 nc.scalar.activation(out=roots[:, 1:], in_=sums_ps[:], func=ACT.Sqrt)

@@ -22,8 +22,12 @@ H_TILES = HID_D // P
 ROW_TILES = B_TILES + H_TILES
 D_TILES = EMB_D // P
 J_TILES = N_NEG // P
-VECTOR_J_TILE = 0
-STATS = 6
+PROD = N_NEG // 2
+PROD_J_TILES = PROD // P
+CLIP_J_TILES = J_TILES - PROD_J_TILES
+CLIP = N_NEG - PROD
+TILE_SLOTS = 28
+LAG = 8
 PSUM_BANKS = 8
 PER_BANK = 4
 
@@ -46,7 +50,8 @@ def tile_hypernymvisual_acc_k_kernel(
         nc.scalar.activation(out=one_root[:], in_=one[:], func=ACT.Sqrt)
 
         emb_t = keep.tile([P, D_TILES, B], F32)
-        neg_t = keep.tile([P, D_TILES, N_NEG], F32)
+        neg_bf = keep.tile([P, D_TILES, PROD], BF16)
+        neg_t = keep.tile([P, D_TILES, CLIP], F32)
         pos_t = keep.tile([P, D_TILES, B], F32)
 
         with (
@@ -193,7 +198,8 @@ def tile_hypernymvisual_acc_k_kernel(
                             identity=ident_bf[:],
                         )
                 copy_out = nc.scalar.copy if first_dt == 0 else nc.vector.tensor_copy
-                copy_out(out=neg_t[:, first_dt : first_dt + 2, :], in_=neg_ps[:])
+                copy_out(out=neg_bf[:, first_dt : first_dt + 2, :], in_=neg_ps[:, :, 0:PROD])
+                copy_out(out=neg_t[:, first_dt : first_dt + 2, :], in_=neg_ps[:, :, PROD:])
             pos_ps = bank_psum.tile([P, D_TILES, B], BF16, tag="bank")
             for dt in range(D_TILES):
                 for bt in range(B_TILES):
@@ -262,14 +268,16 @@ def tile_hypernymvisual_acc_k_kernel(
                 add_bias(first_dt, emb_t, emb_ps, H_TILES)
 
         with (
-            tc.tile_pool(name="clipped", bufs=4) as clipped_pool,
+            tc.tile_pool(name="clipped", bufs=6) as clipped_pool,
+            tc.tile_pool(name="maxima", bufs=2) as maxima_pool,
             tc.tile_pool(name="scratch", bufs=2) as scratch,
-            tc.psum_pool(name="vector_psum", bufs=2) as vector_psum,
-            tc.psum_pool(name="scalar_psum", bufs=PSUM_BANKS - 2) as scalar_psum,
+            tc.psum_pool(name="row_psum", bufs=2) as row_psum,
+            tc.psum_pool(name="col_psum", bufs=2) as col_psum,
+            tc.psum_pool(name="scalar_psum", bufs=PSUM_BANKS - 4) as scalar_psum,
         ):
 
-            def transpose_four(pool, source, cols):
-                bank = pool.tile([P, PER_BANK * P], F32, tag="bank")
+            def transpose_four(source, cols):
+                bank = scalar_psum.tile([P, PER_BANK * P], F32, tag="bank")
                 for t in range(PER_BANK):
                     nc.tensor.transpose(
                         out=bank[:, t * P : (t + 1) * P],
@@ -282,10 +290,50 @@ def tile_hypernymvisual_acc_k_kernel(
                 squares = scratch.tile([P, EMB_D], F32, tag="squares")
                 nc.scalar.activation(out=squares[:], in_=bank[:], func=ACT.Square, accum_out=sum_col)
 
-            sums = keep.tile([P, J_TILES, B], F32)
+            parts = keep.tile([P, 2, D_TILES, B], BF16)
+            low = keep.tile([P, D_TILES, B], F32)
+            for dt in range(D_TILES):
+                nc.scalar.copy(out=parts[:, 0, dt, :], in_=emb_t[:, dt, :])
 
-            def clip_and_transpose(i):
-                clipped = clipped_pool.tile([P, D_TILES, N_NEG], F32, tag="clipped")
+            def split_low():
+                nc.vector.tensor_tensor(out=low[:], in0=emb_t[:], in1=parts[:, 0], op=ALU.subtract)
+                nc.scalar.activation(out=parts[:, 1], in_=low[:], func=ACT.Copy, scale=2.0)
+
+            sums = keep.tile([P, J_TILES, B], F32)
+            by_row = keep.tile([P, B_TILES, PROD], F32)
+            emb_squares = keep.tile([P, B_TILES], F32)
+            pos_sums = keep.tile([P, B_TILES], F32)
+
+            def start_by_row():
+                for bt in range(B_TILES):
+                    i_cols = slice(bt * P, (bt + 1) * P)
+                    scalar_sum_of_squares(transpose_four(emb_t, i_cols), emb_squares[:, bt : bt + 1])
+                    bank = col_psum.tile([P, 2, PROD], F32, tag="col")
+                    for dt in range(D_TILES):
+                        nc.tensor.matmul(
+                            out=bank[:, 0, :],
+                            lhsT=parts[:, 0, dt, i_cols],
+                            rhs=neg_bf[:, dt, :],
+                            start=(dt == 0),
+                            stop=(dt == D_TILES - 1),
+                        )
+                    nc.scalar.activation(
+                        out=by_row[:, bt, :], in_=bank[:, 0, :], func=ACT.Identity,
+                        scale=-1.0, bias=emb_squares[:, bt : bt + 1],
+                    )
+
+            def positives():
+                pos_clipped = keep.tile([P, D_TILES, B], F32)
+                nc.vector.tensor_tensor(out=pos_clipped[:], in0=pos_t[:], in1=emb_t[:], op=ALU.subtract)
+                nc.vector.tensor_scalar_max(out=pos_clipped[:], in0=pos_clipped[:], scalar1=0.0)
+                for bt in range(B_TILES):
+                    scalar_sum_of_squares(
+                        transpose_four(pos_clipped, slice(bt * P, (bt + 1) * P)),
+                        pos_sums[:, bt : bt + 1],
+                    )
+
+            def clip(i):
+                clipped = clipped_pool.tile([P, D_TILES, CLIP], F32, tag="clipped")
                 for dt in range(D_TILES):
                     nc.vector.tensor_scalar(
                         out=clipped[:, dt, :],
@@ -295,61 +343,109 @@ def tile_hypernymvisual_acc_k_kernel(
                         op0=ALU.subtract,
                         op1=ALU.max,
                     )
-                vector_bank = None
-                for jt in range(J_TILES):
-                    j_cols = slice(jt * P, (jt + 1) * P)
-                    if jt == VECTOR_J_TILE:
-                        vector_bank = transpose_four(vector_psum, clipped, j_cols)
-                    else:
-                        scalar_sum_of_squares(
-                            transpose_four(scalar_psum, clipped, j_cols), sums[:, jt, i : i + 1]
-                        )
-                return vector_bank
+                for jt in range(CLIP_J_TILES):
+                    bank = transpose_four(clipped, slice(jt * P, (jt + 1) * P))
+                    scalar_sum_of_squares(bank, sums[:, PROD_J_TILES + jt, i : i + 1])
 
-            stats = keep.tile([P, B, STATS], F32)
-            bank_before = None
-            for i in range(B):
-                vector_bank = clip_and_transpose(i)
-                if bank_before is not None:
-                    nc.vector.bn_stats(out=stats[:, i - 1, :], in_=bank_before[:])
-                bank_before = vector_bank
-            nc.vector.bn_stats(out=stats[:, B - 1, :], in_=bank_before[:])
+            def add_row_bank(bt, dt, bank):
+                i_cols = slice(bt * P, (bt + 1) * P)
+                target = sums[:, 0:PROD_J_TILES, i_cols]
+                if dt == 0:
+                    nc.vector.tensor_reduce(out=target, in_=bank[:], axis=mybir.AxisListType.X, op=ALU.add)
+                else:
+                    both = scratch.tile([P, PROD_J_TILES, P], F32, tag="both")
+                    nc.vector.tensor_reduce(out=both[:], in_=bank[:], axis=mybir.AxisListType.X, op=ALU.add)
+                    nc.vector.tensor_tensor(out=target, in0=target, in1=both[:], op=ALU.add)
 
-            halves = stats[:].rearrange("p i (h k) -> p i h k", k=STATS // 2)
-            mean_squares = keep.tile([P, B, 2], F32)
-            nc.vector.tensor_tensor(
-                out=mean_squares[:], in0=halves[:, :, :, 1], in1=halves[:, :, :, 1], op=ALU.mult
-            )
-            half_sums = keep.tile([P, B, 2], F32)
-            nc.vector.scalar_tensor_tensor(
-                out=half_sums[:],
-                in0=mean_squares[:],
-                scalar=float(EMB_D // 2),
-                in1=halves[:, :, :, 2],
-                op0=ALU.mult,
-                op1=ALU.add,
-            )
-            nc.vector.tensor_tensor(
-                out=sums[:, VECTOR_J_TILE, :], in0=half_sums[:, :, 0], in1=half_sums[:, :, 1],
-                op=ALU.add,
-            )
-
-            pos_clipped = keep.tile([P, D_TILES, B], F32)
-            nc.vector.tensor_tensor(out=pos_clipped[:], in0=pos_t[:], in1=emb_t[:], op=ALU.subtract)
-            nc.vector.tensor_scalar_max(out=pos_clipped[:], in0=pos_clipped[:], scalar1=0.0)
-            pos_sums = keep.tile([P, B_TILES], F32)
-            for bt in range(B_TILES):
-                scalar_sum_of_squares(
-                    transpose_four(scalar_psum, pos_clipped, slice(bt * P, (bt + 1) * P)),
-                    pos_sums[:, bt : bt + 1],
+            def add_col_bank(bt, bank):
+                nc.vector.tensor_tensor(
+                    out=by_row[:, bt, :], in0=by_row[:, bt, :], in1=bank[:, 0, :], op=ALU.add
                 )
 
-            for bt in range(B_TILES):
+            def finish_read(bt):
                 i_cols = slice(bt * P, (bt + 1) * P)
-                sums_ps = transpose_four(scalar_psum, sums, i_cols)
+                sums_ps = transpose_four(sums, i_cols)
                 roots = scratch.tile([P, 1 + N_NEG], F32, tag="roots")
+                turned = scratch.tile([P, PROD], F32, tag="turned")
+                nc.scalar.copy(out=turned[:], in_=sums_ps[:, 0:PROD])
                 nc.scalar.activation(out=roots[:, 0:1], in_=pos_sums[:, bt : bt + 1], func=ACT.Sqrt)
-                nc.scalar.activation(out=roots[:, 1:], in_=sums_ps[:], func=ACT.Sqrt)
+                nc.scalar.activation(out=roots[:, 1 + PROD :], in_=sums_ps[:, PROD:], func=ACT.Sqrt)
+                return bt, roots, turned
+
+            def finish_store(bt, roots, turned):
+                i_cols = slice(bt * P, (bt + 1) * P)
+                nc.vector.tensor_tensor(out=turned[:], in0=by_row[:, bt, :], in1=turned[:], op=ALU.subtract)
+                nc.vector.tensor_scalar_max(out=turned[:], in0=turned[:], scalar1=0.0)
+                nc.scalar.activation(out=roots[:, 1 : 1 + PROD], in_=turned[:], func=ACT.Sqrt)
                 scores = scratch.tile([P, 1 + N_NEG], F32, tag="scores")
                 nc.vector.tensor_scalar_mul(out=scores[:], in0=roots[:], scalar1=-1.0)
                 nc.sync.dma_start(out=out[i_cols, :], in_=scores[:])
+
+            tiles = [(bt, dt) for bt in range(B_TILES) for dt in range(D_TILES)]
+            later = {}
+
+            def at(slot, *call):
+                later.setdefault(slot, []).append(call)
+
+            at(0, split_low)
+            at(6, start_by_row)
+            at(12, positives)
+            maxima = {}
+            row_banks = {}
+            finish_slot = B_TILES * D_TILES * TILE_SLOTS // 2 + TILE_SLOTS + LAG + 1
+
+            def begin_finish():
+                at(finish_slot + LAG, finish_store, *finish_read(0))
+
+            at(finish_slot, begin_finish)
+            pending_rows = []
+            for slot in range(B + 1):
+                if slot < B:
+                    clip(slot)
+                n, k = divmod(slot, TILE_SLOTS)
+                for r, i in pending_rows:
+                    bt, dt = tiles[r]
+                    for jt in range(PROD_J_TILES):
+                        nc.tensor.matmul(
+                            out=row_banks[r][:, jt, i, :],
+                            lhsT=maxima[r][:, i, jt * P : (jt + 1) * P],
+                            rhs=parts[:, :, dt, bt * P + i],
+                            start=True,
+                            stop=True,
+                        )
+                    if i == P - 1:
+                        at(slot + LAG, add_row_bank, bt, dt, row_banks[r])
+                pending_rows = []
+                if n < len(tiles):
+                    bt, dt = tiles[n]
+                    if k == 0:
+                        maxima[n] = maxima_pool.tile([P, P, PROD], BF16, tag="maxima", name="maxima%d" % n)
+                        row_banks[n] = row_psum.tile(
+                            [P, PROD_J_TILES, P, 2], F32, tag="row", name="row_bank%d" % n
+                        )
+                    for i in range(P * k // TILE_SLOTS, P * (k + 1) // TILE_SLOTS):
+                        nc.vector.tensor_scalar(
+                            out=maxima[n][:, i, :],
+                            in0=neg_bf[:, dt, :],
+                            scalar1=parts[:, 0, dt, bt * P + i : bt * P + i + 1],
+                            scalar2=None,
+                            op0=ALU.max,
+                        )
+                        pending_rows.append((n, i))
+                if 1 <= n <= len(tiles):
+                    bt, dt = tiles[n - 1]
+                    if k == 0:
+                        col_bank = col_psum.tile([P, 2, PROD], F32, tag="col")
+                    for j in range(PROD * k // TILE_SLOTS, PROD * (k + 1) // TILE_SLOTS):
+                        nc.tensor.matmul(
+                            out=col_bank[:, 0, j : j + 1],
+                            lhsT=maxima[n - 1][:, :, j],
+                            rhs=neg_bf[:, dt, j : j + 1],
+                            start=True,
+                            stop=True,
+                        )
+                    if k == TILE_SLOTS - 1:
+                        at(min(slot + LAG, B), add_col_bank, bt, col_bank)
+                for call in later.pop(slot, []):
+                    call[0](*call[1:])
+            finish_store(*finish_read(1))

@@ -26,8 +26,6 @@ PROD = N_NEG // 2
 PROD_J_TILES = PROD // P
 CLIP_J_TILES = J_TILES - PROD_J_TILES
 CLIP = N_NEG - PROD
-TILE_SLOTS = 28
-LAG = 8
 PSUM_BANKS = 8
 PER_BANK = 4
 
@@ -269,11 +267,10 @@ def tile_hypernymvisual_acc_k_kernel(
 
         with (
             tc.tile_pool(name="clipped", bufs=6) as clipped_pool,
-            tc.tile_pool(name="maxima", bufs=2) as maxima_pool,
+            tc.tile_pool(name="maxima", bufs=6) as maxima_pool,
             tc.tile_pool(name="scratch", bufs=2) as scratch,
-            tc.psum_pool(name="row_psum", bufs=2) as row_psum,
-            tc.psum_pool(name="col_psum", bufs=2) as col_psum,
-            tc.psum_pool(name="scalar_psum", bufs=PSUM_BANKS - 4) as scalar_psum,
+            tc.psum_pool(name="prod_psum", bufs=1) as prod_psum,
+            tc.psum_pool(name="scalar_psum", bufs=PSUM_BANKS - 3) as scalar_psum,
         ):
 
             def transpose_four(source, cols):
@@ -304,21 +301,27 @@ def tile_hypernymvisual_acc_k_kernel(
             emb_squares = keep.tile([P, B_TILES], F32)
             pos_sums = keep.tile([P, B_TILES], F32)
 
+            row_banks = [
+                prod_psum.tile([P, PROD_J_TILES, P, 2], F32, name="row_bank%d" % bt)
+                for bt in range(B_TILES)
+            ]
+            col_bank = prod_psum.tile([P, B_TILES, PROD], F32, name="col_bank")
+
             def start_by_row():
                 for bt in range(B_TILES):
                     i_cols = slice(bt * P, (bt + 1) * P)
                     scalar_sum_of_squares(transpose_four(emb_t, i_cols), emb_squares[:, bt : bt + 1])
-                    bank = col_psum.tile([P, 2, PROD], F32, tag="col")
+                    bank = scalar_psum.tile([P, PER_BANK * P], F32, tag="bank")
                     for dt in range(D_TILES):
                         nc.tensor.matmul(
-                            out=bank[:, 0, :],
+                            out=bank[:, 0:PROD],
                             lhsT=parts[:, 0, dt, i_cols],
                             rhs=neg_bf[:, dt, :],
                             start=(dt == 0),
                             stop=(dt == D_TILES - 1),
                         )
                     nc.scalar.activation(
-                        out=by_row[:, bt, :], in_=bank[:, 0, :], func=ACT.Identity,
+                        out=by_row[:, bt, :], in_=bank[:, 0:PROD], func=ACT.Identity,
                         scale=-1.0, bias=emb_squares[:, bt : bt + 1],
                     )
 
@@ -347,105 +350,83 @@ def tile_hypernymvisual_acc_k_kernel(
                     bank = transpose_four(clipped, slice(jt * P, (jt + 1) * P))
                     scalar_sum_of_squares(bank, sums[:, PROD_J_TILES + jt, i : i + 1])
 
-            def add_row_bank(bt, dt, bank):
-                i_cols = slice(bt * P, (bt + 1) * P)
-                target = sums[:, 0:PROD_J_TILES, i_cols]
-                if dt == 0:
-                    nc.vector.tensor_reduce(out=target, in_=bank[:], axis=mybir.AxisListType.X, op=ALU.add)
-                else:
-                    both = scratch.tile([P, PROD_J_TILES, P], F32, tag="both")
-                    nc.vector.tensor_reduce(out=both[:], in_=bank[:], axis=mybir.AxisListType.X, op=ALU.add)
-                    nc.vector.tensor_tensor(out=target, in0=target, in1=both[:], op=ALU.add)
+            def maxima_of(source, scalars, index):
+                maxima = maxima_pool.tile([P, D_TILES, PROD], BF16, tag="maxima")
+                for dt in range(D_TILES):
+                    nc.vector.tensor_scalar(
+                        out=maxima[:, dt, :],
+                        in0=source[:, dt, :],
+                        scalar1=scalars[:, dt, index : index + 1],
+                        scalar2=None,
+                        op0=ALU.max,
+                    )
+                return maxima
 
-            def add_col_bank(bt, bank):
-                nc.vector.tensor_tensor(
-                    out=by_row[:, bt, :], in0=by_row[:, bt, :], in1=bank[:, 0, :], op=ALU.add
+            high = parts[:, 0]
+
+            def row_products(i, maxima):
+                bt, r = divmod(i, P)
+                for jt in range(PROD_J_TILES):
+                    for dt in range(D_TILES):
+                        nc.tensor.matmul(
+                            out=row_banks[bt][:, jt, r, :],
+                            lhsT=maxima[:, dt, jt * P : (jt + 1) * P],
+                            rhs=parts[:, :, dt, i],
+                            start=(dt == 0),
+                            stop=(dt == D_TILES - 1),
+                        )
+
+            def column_products(j, maxima):
+                for bt in range(B_TILES):
+                    for dt in range(D_TILES):
+                        nc.tensor.matmul(
+                            out=col_bank[:, bt, j : j + 1],
+                            lhsT=maxima[:, dt, bt * P : (bt + 1) * P],
+                            rhs=neg_bf[:, dt, j : j + 1],
+                            start=(dt == 0),
+                            stop=(dt == D_TILES - 1),
+                        )
+
+            def add_row_products(bt):
+                nc.vector.tensor_reduce(
+                    out=sums[:, 0:PROD_J_TILES, bt * P : (bt + 1) * P], in_=row_banks[bt][:],
+                    axis=mybir.AxisListType.X, op=ALU.add,
                 )
 
-            def finish_read(bt):
+            def finish(bt):
                 i_cols = slice(bt * P, (bt + 1) * P)
                 sums_ps = transpose_four(sums, i_cols)
                 roots = scratch.tile([P, 1 + N_NEG], F32, tag="roots")
-                turned = scratch.tile([P, PROD], F32, tag="turned")
-                nc.scalar.copy(out=turned[:], in_=sums_ps[:, 0:PROD])
+                prod_sums = scratch.tile([P, PROD], F32, tag="prod_sums")
                 nc.scalar.activation(out=roots[:, 0:1], in_=pos_sums[:, bt : bt + 1], func=ACT.Sqrt)
                 nc.scalar.activation(out=roots[:, 1 + PROD :], in_=sums_ps[:, PROD:], func=ACT.Sqrt)
-                return bt, roots, turned
-
-            def finish_store(bt, roots, turned):
-                i_cols = slice(bt * P, (bt + 1) * P)
-                nc.vector.tensor_tensor(out=turned[:], in0=by_row[:, bt, :], in1=turned[:], op=ALU.subtract)
-                nc.vector.tensor_scalar_max(out=turned[:], in0=turned[:], scalar1=0.0)
-                nc.scalar.activation(out=roots[:, 1 : 1 + PROD], in_=turned[:], func=ACT.Sqrt)
+                nc.vector.tensor_tensor(
+                    out=prod_sums[:], in0=by_row[:, bt, :], in1=sums_ps[:, 0:PROD], op=ALU.subtract
+                )
+                nc.vector.tensor_scalar_max(out=prod_sums[:], in0=prod_sums[:], scalar1=0.0)
+                nc.scalar.activation(out=roots[:, 1 : 1 + PROD], in_=prod_sums[:], func=ACT.Sqrt)
                 scores = scratch.tile([P, 1 + N_NEG], F32, tag="scores")
                 nc.vector.tensor_scalar_mul(out=scores[:], in0=roots[:], scalar1=-1.0)
                 nc.sync.dma_start(out=out[i_cols, :], in_=scores[:])
 
-            tiles = [(bt, dt) for bt in range(B_TILES) for dt in range(D_TILES)]
-            later = {}
-
-            def at(slot, *call):
-                later.setdefault(slot, []).append(call)
-
-            at(0, split_low)
-            at(6, start_by_row)
-            at(12, positives)
-            maxima = {}
-            row_banks = {}
-            finish_slot = B_TILES * D_TILES * TILE_SLOTS // 2 + TILE_SLOTS + LAG + 1
-
-            def begin_finish():
-                at(finish_slot + LAG, finish_store, *finish_read(0))
-
-            at(finish_slot, begin_finish)
-            pending_rows = []
-            for slot in range(B + 1):
-                if slot < B:
-                    clip(slot)
-                n, k = divmod(slot, TILE_SLOTS)
-                for r, i in pending_rows:
-                    bt, dt = tiles[r]
-                    for jt in range(PROD_J_TILES):
-                        nc.tensor.matmul(
-                            out=row_banks[r][:, jt, i, :],
-                            lhsT=maxima[r][:, i, jt * P : (jt + 1) * P],
-                            rhs=parts[:, :, dt, bt * P + i],
-                            start=True,
-                            stop=True,
-                        )
-                    if i == P - 1:
-                        at(slot + LAG, add_row_bank, bt, dt, row_banks[r])
-                pending_rows = []
-                if n < len(tiles):
-                    bt, dt = tiles[n]
-                    if k == 0:
-                        maxima[n] = maxima_pool.tile([P, P, PROD], BF16, tag="maxima", name="maxima%d" % n)
-                        row_banks[n] = row_psum.tile(
-                            [P, PROD_J_TILES, P, 2], F32, tag="row", name="row_bank%d" % n
-                        )
-                    for i in range(P * k // TILE_SLOTS, P * (k + 1) // TILE_SLOTS):
-                        nc.vector.tensor_scalar(
-                            out=maxima[n][:, i, :],
-                            in0=neg_bf[:, dt, :],
-                            scalar1=parts[:, 0, dt, bt * P + i : bt * P + i + 1],
-                            scalar2=None,
-                            op0=ALU.max,
-                        )
-                        pending_rows.append((n, i))
-                if 1 <= n <= len(tiles):
-                    bt, dt = tiles[n - 1]
-                    if k == 0:
-                        col_bank = col_psum.tile([P, 2, PROD], F32, tag="col")
-                    for j in range(PROD * k // TILE_SLOTS, PROD * (k + 1) // TILE_SLOTS):
-                        nc.tensor.matmul(
-                            out=col_bank[:, 0, j : j + 1],
-                            lhsT=maxima[n - 1][:, :, j],
-                            rhs=neg_bf[:, dt, j : j + 1],
-                            start=True,
-                            stop=True,
-                        )
-                    if k == TILE_SLOTS - 1:
-                        at(min(slot + LAG, B), add_col_bank, bt, col_bank)
-                for call in later.pop(slot, []):
-                    call[0](*call[1:])
-            finish_store(*finish_read(1))
+            before = None
+            for i in range(B):
+                clip(i)
+                if before is not None:
+                    row_products(i - 1, before[0])
+                    column_products(i - 1, before[1])
+                before = (maxima_of(neg_bf, high, i), maxima_of(high, neg_bf, i))
+                if i == 0:
+                    split_low()
+                elif i == 6:
+                    start_by_row()
+                elif i == 12:
+                    positives()
+                elif i == P + 8:
+                    add_row_products(0)
+            row_products(B - 1, before[0])
+            column_products(B - 1, before[1])
+            add_row_products(1)
+            nc.vector.tensor_tensor(out=by_row[:], in0=by_row[:], in1=col_bank[:], op=ALU.add)
+            for bt in range(B_TILES):
+                finish(bt)

@@ -24,8 +24,12 @@ D_TILES = EMB_D // P
 J_TILES = N_NEG // P
 PROD = N_NEG // 2
 PROD_J_TILES = PROD // P
-CLIP_J_TILES = J_TILES - PROD_J_TILES
-CLIP = N_NEG - PROD
+SQ = N_NEG - PROD
+RUN = 2
+LEAD = 4
+BANK_ROWS = 64
+VECTOR_PERIOD = 16
+STATS = 6
 PSUM_BANKS = 8
 PER_BANK = 4
 
@@ -48,8 +52,8 @@ def tile_hypernymvisual_acc_k_kernel(
         nc.scalar.activation(out=one_root[:], in_=one[:], func=ACT.Sqrt)
 
         emb_t = keep.tile([P, D_TILES, B], F32)
-        neg_bf = keep.tile([P, D_TILES, PROD], BF16)
-        neg_t = keep.tile([P, D_TILES, CLIP], F32)
+        neg_bf = keep.tile([P, D_TILES, N_NEG], BF16)
+        neg_t = keep.tile([P, D_TILES, PROD], F32)
         pos_t = keep.tile([P, D_TILES, B], F32)
 
         with (
@@ -196,8 +200,8 @@ def tile_hypernymvisual_acc_k_kernel(
                             identity=ident_bf[:],
                         )
                 copy_out = nc.scalar.copy if first_dt == 0 else nc.vector.tensor_copy
-                copy_out(out=neg_bf[:, first_dt : first_dt + 2, :], in_=neg_ps[:, :, 0:PROD])
-                copy_out(out=neg_t[:, first_dt : first_dt + 2, :], in_=neg_ps[:, :, PROD:])
+                copy_out(out=neg_bf[:, first_dt : first_dt + 2, :], in_=neg_ps[:])
+                copy_out(out=neg_t[:, first_dt : first_dt + 2, :], in_=neg_ps[:, :, 0:PROD])
             pos_ps = bank_psum.tile([P, D_TILES, B], BF16, tag="bank")
             for dt in range(D_TILES):
                 for bt in range(B_TILES):
@@ -266,15 +270,16 @@ def tile_hypernymvisual_acc_k_kernel(
                 add_bias(first_dt, emb_t, emb_ps, H_TILES)
 
         with (
-            tc.tile_pool(name="clipped", bufs=6) as clipped_pool,
-            tc.tile_pool(name="maxima", bufs=6) as maxima_pool,
+            tc.tile_pool(name="row_maxima", bufs=2 * LEAD + 2) as row_pool,
+            tc.tile_pool(name="col_maxima", bufs=2 * LEAD + 2) as col_pool,
             tc.tile_pool(name="scratch", bufs=2) as scratch,
-            tc.psum_pool(name="prod_psum", bufs=1) as prod_psum,
-            tc.psum_pool(name="scalar_psum", bufs=PSUM_BANKS - 3) as scalar_psum,
+            tc.psum_pool(name="col_psum", bufs=1) as col_psum,
+            tc.psum_pool(name="row_psum", bufs=2) as row_psum,
+            tc.psum_pool(name="turn_psum", bufs=PSUM_BANKS - 3) as turn_psum,
         ):
 
             def transpose_four(source, cols):
-                bank = scalar_psum.tile([P, PER_BANK * P], F32, tag="bank")
+                bank = turn_psum.tile([P, PER_BANK * P], F32, tag="bank")
                 for t in range(PER_BANK):
                     nc.tensor.transpose(
                         out=bank[:, t * P : (t + 1) * P],
@@ -283,40 +288,41 @@ def tile_hypernymvisual_acc_k_kernel(
                     )
                 return bank
 
-            def scalar_sum_of_squares(bank, sum_col):
+            def scalar_sum_of_squares(values, sum_col):
                 squares = scratch.tile([P, EMB_D], F32, tag="squares")
-                nc.scalar.activation(out=squares[:], in_=bank[:], func=ACT.Square, accum_out=sum_col)
+                nc.scalar.activation(out=squares[:], in_=values, func=ACT.Square, accum_out=sum_col)
 
             parts = keep.tile([P, 2, D_TILES, B], BF16)
+            high = parts[:, 0]
+            high_f32 = keep.tile([P, D_TILES, B], F32)
             low = keep.tile([P, D_TILES, B], F32)
             for dt in range(D_TILES):
                 nc.scalar.copy(out=parts[:, 0, dt, :], in_=emb_t[:, dt, :])
+            for dt in range(D_TILES):
+                nc.scalar.copy(out=high_f32[:, dt, :], in_=parts[:, 0, dt, :])
 
             def split_low():
-                nc.vector.tensor_tensor(out=low[:], in0=emb_t[:], in1=parts[:, 0], op=ALU.subtract)
+                nc.vector.tensor_tensor(out=low[:], in0=emb_t[:], in1=high_f32[:], op=ALU.subtract)
                 nc.scalar.activation(out=parts[:, 1], in_=low[:], func=ACT.Copy, scale=2.0)
 
-            sums = keep.tile([P, J_TILES, B], F32)
+            row_sums = keep.tile([P, J_TILES, B], F32)
+            square_sums = keep.tile([P, 2, B], F32)
             by_row = keep.tile([P, B_TILES, PROD], F32)
             emb_squares = keep.tile([P, B_TILES], F32)
             pos_sums = keep.tile([P, B_TILES], F32)
-
-            row_banks = [
-                prod_psum.tile([P, PROD_J_TILES, P, 2], F32, name="row_bank%d" % bt)
-                for bt in range(B_TILES)
-            ]
-            col_bank = prod_psum.tile([P, B_TILES, PROD], F32, name="col_bank")
+            stats = keep.tile([P, B // VECTOR_PERIOD, 2, STATS], F32)
+            col_bank = col_psum.tile([P, B_TILES, PROD], F32, name="col_bank")
 
             def start_by_row():
                 for bt in range(B_TILES):
                     i_cols = slice(bt * P, (bt + 1) * P)
-                    scalar_sum_of_squares(transpose_four(emb_t, i_cols), emb_squares[:, bt : bt + 1])
-                    bank = scalar_psum.tile([P, PER_BANK * P], F32, tag="bank")
+                    scalar_sum_of_squares(transpose_four(emb_t, i_cols)[:], emb_squares[:, bt : bt + 1])
+                    bank = turn_psum.tile([P, PER_BANK * P], F32, tag="bank")
                     for dt in range(D_TILES):
                         nc.tensor.matmul(
                             out=bank[:, 0:PROD],
                             lhsT=parts[:, 0, dt, i_cols],
-                            rhs=neg_bf[:, dt, :],
+                            rhs=neg_bf[:, dt, 0:PROD],
                             start=(dt == 0),
                             stop=(dt == D_TILES - 1),
                         )
@@ -331,27 +337,12 @@ def tile_hypernymvisual_acc_k_kernel(
                 nc.vector.tensor_scalar_max(out=pos_clipped[:], in0=pos_clipped[:], scalar1=0.0)
                 for bt in range(B_TILES):
                     scalar_sum_of_squares(
-                        transpose_four(pos_clipped, slice(bt * P, (bt + 1) * P)),
+                        transpose_four(pos_clipped, slice(bt * P, (bt + 1) * P))[:],
                         pos_sums[:, bt : bt + 1],
                     )
 
-            def clip(i):
-                clipped = clipped_pool.tile([P, D_TILES, CLIP], F32, tag="clipped")
-                for dt in range(D_TILES):
-                    nc.vector.tensor_scalar(
-                        out=clipped[:, dt, :],
-                        in0=neg_t[:, dt, :],
-                        scalar1=emb_t[:, dt, i : i + 1],
-                        scalar2=0.0,
-                        op0=ALU.subtract,
-                        op1=ALU.max,
-                    )
-                for jt in range(CLIP_J_TILES):
-                    bank = transpose_four(clipped, slice(jt * P, (jt + 1) * P))
-                    scalar_sum_of_squares(bank, sums[:, PROD_J_TILES + jt, i : i + 1])
-
-            def maxima_of(source, scalars, index):
-                maxima = maxima_pool.tile([P, D_TILES, PROD], BF16, tag="maxima")
+            def maxima_of(pool, source, scalars, index):
+                maxima = pool.tile([P, D_TILES, source.shape[2]], BF16, tag="maxima")
                 for dt in range(D_TILES):
                     nc.vector.tensor_scalar(
                         out=maxima[:, dt, :],
@@ -362,14 +353,21 @@ def tile_hypernymvisual_acc_k_kernel(
                     )
                 return maxima
 
-            high = parts[:, 0]
+            def turn(maxima):
+                bank = turn_psum.tile([P, PER_BANK * P], F32, tag="bank")
+                for dt in range(D_TILES):
+                    nc.tensor.transpose(
+                        out=bank[:, dt * P : (dt + 1) * P],
+                        in_=maxima[:, dt, PROD:].bitcast(F32),
+                        identity=ident_f32[:],
+                    )
+                return bank
 
-            def row_products(i, maxima):
-                bt, r = divmod(i, P)
-                for jt in range(PROD_J_TILES):
+            def row_products(i, maxima, bank):
+                for jt in range(J_TILES):
                     for dt in range(D_TILES):
                         nc.tensor.matmul(
-                            out=row_banks[bt][:, jt, r, :],
+                            out=bank[:, jt, i % BANK_ROWS, :],
                             lhsT=maxima[:, dt, jt * P : (jt + 1) * P],
                             rhs=parts[:, :, dt, i],
                             start=(dt == 0),
@@ -387,46 +385,113 @@ def tile_hypernymvisual_acc_k_kernel(
                             stop=(dt == D_TILES - 1),
                         )
 
-            def add_row_products(bt):
+            def sum_squares(i, bank):
+                values = bank[:].bitcast(BF16).rearrange("p (d e) -> p e d", e=2)
+                for e in range(2):
+                    if i % VECTOR_PERIOD == VECTOR_PERIOD - 1:
+                        nc.vector.bn_stats(out=stats[:, i // VECTOR_PERIOD, e, :], in_=values[:, e, :])
+                    else:
+                        scalar_sum_of_squares(values[:, e, :], square_sums[:, e, i : i + 1])
+
+            def add_row_products(first_row, bank):
+                i_cols = slice(first_row, first_row + BANK_ROWS)
+                again = scratch.tile([P, J_TILES - PROD_J_TILES, BANK_ROWS], F32, tag="again")
+                nc.scalar.copy(out=again[:], in_=bank[:, PROD_J_TILES:, :, 0])
                 nc.vector.tensor_reduce(
-                    out=sums[:, 0:PROD_J_TILES, bt * P : (bt + 1) * P], in_=row_banks[bt][:],
-                    axis=mybir.AxisListType.X, op=ALU.add,
+                    out=row_sums[:, :, i_cols], in_=bank[:], axis=mybir.AxisListType.X, op=ALU.add
                 )
+                nc.vector.tensor_tensor(
+                    out=row_sums[:, PROD_J_TILES:, i_cols],
+                    in0=row_sums[:, PROD_J_TILES:, i_cols],
+                    in1=again[:],
+                    op=ALU.add,
+                )
+
+            def sums_from_stats():
+                halves = stats[:].rearrange("p i e (h k) -> p i e h k", k=STATS // 2)
+                mean_squares = keep.tile([P, B // VECTOR_PERIOD, 2, 2], F32)
+                nc.vector.tensor_tensor(
+                    out=mean_squares[:], in0=halves[:, :, :, :, 1], in1=halves[:, :, :, :, 1], op=ALU.mult
+                )
+                half_sums = keep.tile([P, B // VECTOR_PERIOD, 2, 2], F32)
+                nc.vector.scalar_tensor_tensor(
+                    out=half_sums[:],
+                    in0=mean_squares[:],
+                    scalar=float(EMB_D // 2),
+                    in1=halves[:, :, :, :, 2],
+                    op0=ALU.mult,
+                    op1=ALU.add,
+                )
+                for e in range(2):
+                    nc.vector.tensor_tensor(
+                        out=square_sums[:, e, VECTOR_PERIOD - 1 :: VECTOR_PERIOD],
+                        in0=half_sums[:, :, e, 0],
+                        in1=half_sums[:, :, e, 1],
+                        op=ALU.add,
+                    )
 
             def finish(bt):
                 i_cols = slice(bt * P, (bt + 1) * P)
-                sums_ps = transpose_four(sums, i_cols)
-                roots = scratch.tile([P, 1 + N_NEG], F32, tag="roots")
-                prod_sums = scratch.tile([P, PROD], F32, tag="prod_sums")
-                nc.scalar.activation(out=roots[:, 0:1], in_=pos_sums[:, bt : bt + 1], func=ACT.Sqrt)
-                nc.scalar.activation(out=roots[:, 1 + PROD :], in_=sums_ps[:, PROD:], func=ACT.Sqrt)
-                nc.vector.tensor_tensor(
-                    out=prod_sums[:], in0=by_row[:, bt, :], in1=sums_ps[:, 0:PROD], op=ALU.subtract
+                rows_ps = transpose_four(row_sums, i_cols)
+                squares_ps = turn_psum.tile([P, PER_BANK * P], F32, tag="bank")
+                for e in range(2):
+                    nc.tensor.transpose(
+                        out=squares_ps[:, e * P : (e + 1) * P],
+                        in_=square_sums[:, e, i_cols],
+                        identity=ident_f32[:],
+                    )
+                totals = scratch.tile([P, N_NEG], F32, tag="totals")
+                nc.scalar.activation(
+                    out=totals[:, PROD:].rearrange("p (w e) -> p w e", e=2),
+                    in_=squares_ps[:, 0:SQ].rearrange("p (e w) -> p w e", e=2),
+                    func=ACT.Identity,
+                    bias=emb_squares[:, bt : bt + 1],
                 )
-                nc.vector.tensor_scalar_max(out=prod_sums[:], in0=prod_sums[:], scalar1=0.0)
-                nc.scalar.activation(out=roots[:, 1 : 1 + PROD], in_=prod_sums[:], func=ACT.Sqrt)
+                nc.vector.tensor_tensor(
+                    out=totals[:, 0:PROD], in0=by_row[:, bt, :], in1=rows_ps[:, 0:PROD], op=ALU.subtract
+                )
+                nc.vector.tensor_tensor(
+                    out=totals[:, PROD:], in0=totals[:, PROD:], in1=rows_ps[:, PROD:], op=ALU.subtract
+                )
+                nc.vector.tensor_scalar_max(out=totals[:], in0=totals[:], scalar1=0.0)
+                roots = scratch.tile([P, 1 + N_NEG], F32, tag="roots")
+                nc.scalar.activation(out=roots[:, 0:1], in_=pos_sums[:, bt : bt + 1], func=ACT.Sqrt)
+                nc.scalar.activation(out=roots[:, 1:], in_=totals[:], func=ACT.Sqrt)
                 scores = scratch.tile([P, 1 + N_NEG], F32, tag="scores")
                 nc.vector.tensor_scalar_mul(out=scores[:], in0=roots[:], scalar1=-1.0)
                 nc.sync.dma_start(out=out[i_cols, :], in_=scores[:])
 
-            before = None
-            for i in range(B):
-                clip(i)
-                if before is not None:
-                    row_products(i - 1, before[0])
-                    column_products(i - 1, before[1])
-                before = (maxima_of(neg_bf, high, i), maxima_of(high, neg_bf, i))
-                if i == 0:
+            made = []
+            row_bank = None
+            full_bank = None
+            for step in range(0, B + LEAD, RUN):
+                for i in range(step, min(step + RUN, B)):
+                    row_maxima = maxima_of(row_pool, neg_bf, high_f32, i)
+                    col_maxima = maxima_of(col_pool, high, neg_t, i)
+                    made.append((row_maxima, col_maxima))
+                if step == 0:
                     split_low()
-                elif i == 6:
+                if full_bank is not None:
+                    add_row_products(*full_bank)
+                    full_bank = None
+                if step >= LEAD:
+                    rows = range(step - LEAD, step - LEAD + RUN)
+                    banks = [turn(made[i][0]) for i in rows]
+                    for i in rows:
+                        if i % BANK_ROWS == 0:
+                            row_bank = row_psum.tile([P, J_TILES, BANK_ROWS, 2], F32, tag="row_bank")
+                        row_products(i, made[i][0], row_bank)
+                        column_products(i, made[i][1])
+                        if i % BANK_ROWS == BANK_ROWS - 1:
+                            full_bank = (i + 1 - BANK_ROWS, row_bank)
+                    for i, bank in zip(rows, banks):
+                        sum_squares(i, bank)
+                if step == 8:
                     start_by_row()
-                elif i == 12:
+                elif step == 16:
                     positives()
-                elif i == P + 8:
-                    add_row_products(0)
-            row_products(B - 1, before[0])
-            column_products(B - 1, before[1])
-            add_row_products(1)
+            add_row_products(*full_bank)
+            sums_from_stats()
             nc.vector.tensor_tensor(out=by_row[:], in0=by_row[:], in1=col_bank[:], op=ALU.add)
             for bt in range(B_TILES):
                 finish(bt)

@@ -353,14 +353,25 @@ def tile_hypernymvisual_acc_k_kernel(
                     )
                 return maxima
 
-            def turn(maxima):
-                bank = turn_psum.tile([P, PER_BANK * P], F32, tag="bank")
+            def turn(maxima, bank):
                 for dt in range(D_TILES):
                     nc.tensor.transpose(
                         out=bank[:, dt * P : (dt + 1) * P],
                         in_=maxima[:, dt, PROD:].bitcast(F32),
                         identity=ident_f32[:],
                     )
+
+            def wide_pass():
+                bank = turn_psum.tile([P, PER_BANK * P], F32, tag="bank")
+                nc.tensor.matmul_mx(
+                    out=bank[:],
+                    lhsT=we_codes[:, 0:P].bitcast(FP8X4),
+                    lhsT_scale=we_scales[:, 0:P],
+                    rhs=we_codes[:].bitcast(FP8X4),
+                    rhs_scale=we_scales[:],
+                    start=True,
+                    stop=True,
+                )
                 return bank
 
             def row_products(i, maxima, bank):
@@ -476,7 +487,9 @@ def tile_hypernymvisual_acc_k_kernel(
                     full_bank = None
                 if step >= LEAD:
                     rows = range(step - LEAD, step - LEAD + RUN)
-                    banks = [turn(made[i][0]) for i in rows]
+                    banks = [wide_pass() for i in rows]
+                    for i, bank in zip(rows, banks):
+                        turn(made[i][0], bank)
                     for i in rows:
                         if i % BANK_ROWS == 0:
                             row_bank = row_psum.tile([P, J_TILES, BANK_ROWS, 2], F32, tag="row_bank")

@@ -14,9 +14,12 @@ B, N_NEG, VF_D, HID_D, EMB_D = 256, 512, 16384, 512, 512
 P = 128
 QUAD = 4
 K_PASS = P * QUAD
-K_CHUNK = 2048
-PASSES_PER_CHUNK = K_CHUNK // K_PASS
-CHUNKS = VF_D // K_CHUNK
+PASSES = VF_D // K_PASS
+LOADS = [1, 1, 2] + [4] * 6 + [2, 1, 1]
+MOST_PASSES = max(LOADS)
+LABEL_LOAD = 3
+STEP = 4
+LAG = 2
 B_TILES = B // P
 H_TILES = HID_D // P
 ROW_TILES = B_TILES + H_TILES
@@ -27,8 +30,12 @@ PROD_J_TILES = PROD // P
 SQ = N_NEG - PROD
 RUN = 2
 LEAD = 4
-BANK_ROWS = 64
-VECTOR_PERIOD = 16
+BANK_ROWS = 32
+WIDE = 256
+WIDE_EVERY = 4
+COL_LEAD = 16
+VECTOR_PERIOD = 12
+VECTOR_ROWS = range(VECTOR_PERIOD - 1, B - COL_LEAD, VECTOR_PERIOD)
 STATS = 6
 PSUM_BANKS = 8
 PER_BANK = 4
@@ -52,14 +59,17 @@ def tile_hypernymvisual_acc_k_kernel(
         nc.scalar.activation(out=one_root[:], in_=one[:], func=ACT.Sqrt)
 
         emb_t = keep.tile([P, D_TILES, B], F32)
+        parts = keep.tile([P, 2, D_TILES, B], BF16)
+        high = parts[:, 0]
+        high_f32 = keep.tile([P, D_TILES, B], F32)
         neg_bf = keep.tile([P, D_TILES, N_NEG], BF16)
         neg_t = keep.tile([P, D_TILES, PROD], F32)
         pos_t = keep.tile([P, D_TILES, B], F32)
 
         with (
-            tc.tile_pool(name="load", bufs=3) as load,
+            tc.tile_pool(name="load", bufs=4) as load,
             tc.tile_pool(name="work", bufs=3) as work,
-            tc.tile_pool(name="codes", bufs=2) as codes,
+            tc.tile_pool(name="codes", bufs=STEP + LAG + 2) as codes,
             tc.psum_pool(name="acc_psum", bufs=1) as acc_psum,
             tc.psum_pool(name="bank_psum", bufs=PSUM_BANKS - B_TILES) as bank_psum,
         ):
@@ -104,11 +114,12 @@ def tile_hypernymvisual_acc_k_kernel(
             wh_view = W_hidden.rearrange("(t p) k -> p t k", p=P)
             acc = [acc_psum.tile([P, HID_D], F32, name="acc%d" % bt) for bt in range(B_TILES)]
 
-            def load_chunk(c):
-                rows = load.tile([P, ROW_TILES, K_CHUNK], BF16, tag="rows")
-                k_cols = slice(c * K_CHUNK, (c + 1) * K_CHUNK)
-                nc.sync.dma_start(out=rows[:, 0:B_TILES, :], in_=vf_view[:, :, k_cols])
-                nc.sync.dma_start(out=rows[:, B_TILES:ROW_TILES, :], in_=wh_view[:, :, k_cols])
+            def load_passes(first, count):
+                rows = load.tile([P, ROW_TILES, MOST_PASSES * K_PASS], BF16, tag="rows")
+                width = count * K_PASS
+                k_cols = slice(first * K_PASS, first * K_PASS + width)
+                nc.sync.dma_start(out=rows[:, 0:B_TILES, 0:width], in_=vf_view[:, :, k_cols])
+                nc.sync.dma_start(out=rows[:, B_TILES:ROW_TILES, 0:width], in_=wh_view[:, :, k_cols])
                 return rows
 
             def transpose_pass(rows, g):
@@ -135,84 +146,87 @@ def tile_hypernymvisual_acc_k_kernel(
                 return grouped
 
             def new_codes():
-                vf_codes = codes.tile([P, PASSES_PER_CHUNK, B], U32, tag="vf_codes", align_bytes=64)
-                vf_scales = codes.tile([P, PASSES_PER_CHUNK, B], U8, tag="vf_scales", align_bytes=64)
-                wh_codes = codes.tile([P, PASSES_PER_CHUNK, HID_D], U32, tag="wh_codes", align_bytes=64)
-                wh_scales = codes.tile([P, PASSES_PER_CHUNK, HID_D], U8, tag="wh_scales", align_bytes=64)
+                vf_codes = codes.tile([P, B], U32, tag="vf_codes", align_bytes=64)
+                vf_scales = codes.tile([P, B], U8, tag="vf_scales", align_bytes=64)
+                wh_codes = codes.tile([P, HID_D], U32, tag="wh_codes", align_bytes=64)
+                wh_scales = codes.tile([P, HID_D], U8, tag="wh_scales", align_bytes=64)
                 return vf_codes, vf_scales, wh_codes, wh_scales
 
-            def quantise_pass(grouped, chunk_codes, g):
-                vf_codes, vf_scales, wh_codes, wh_scales = chunk_codes
+            def quantise_pass(grouped, pass_codes):
+                vf_codes, vf_scales, wh_codes, wh_scales = pass_codes
                 vf_end = B * QUAD
                 nc.vector.quantize_mx(
-                    out=vf_codes[:, g, :].bitcast(FP8X4),
-                    scales=vf_scales[:, g, :],
-                    in_=grouped[:, 0:vf_end],
+                    out=vf_codes[:].bitcast(FP8X4), scales=vf_scales[:], in_=grouped[:, 0:vf_end]
                 )
                 nc.vector.quantize_mx(
-                    out=wh_codes[:, g, :].bitcast(FP8X4),
-                    scales=wh_scales[:, g, :],
-                    in_=grouped[:, vf_end:],
+                    out=wh_codes[:].bitcast(FP8X4), scales=wh_scales[:], in_=grouped[:, vf_end:]
                 )
 
-            def multiply_chunk(c, chunk_codes):
-                vf_codes, vf_scales, wh_codes, wh_scales = chunk_codes
-                for g in range(PASSES_PER_CHUNK):
+            def multiply_pass(n, pass_codes):
+                vf_codes, vf_scales, wh_codes, wh_scales = pass_codes
+                for bt in range(B_TILES):
+                    b_cols = slice(bt * P, (bt + 1) * P)
+                    nc.tensor.matmul_mx(
+                        out=acc[bt][:],
+                        lhsT=vf_codes[:, b_cols].bitcast(FP8X4),
+                        lhsT_scale=vf_scales[:, b_cols],
+                        rhs=wh_codes[:].bitcast(FP8X4),
+                        rhs_scale=wh_scales[:],
+                        start=(n == 0),
+                        stop=(n == PASSES - 1),
+                    )
+
+            def transpose_labels(neg_sb, pos_sb):
+                for first_dt in range(0, D_TILES, 2):
+                    neg_ps = bank_psum.tile([P, 2, N_NEG], BF16, tag="bank")
+                    for s in range(2):
+                        d_cols = slice((first_dt + s) * P, (first_dt + s + 1) * P)
+                        for jt in range(J_TILES):
+                            nc.tensor.transpose(
+                                out=neg_ps[:, s, jt * P : (jt + 1) * P],
+                                in_=neg_sb[:, jt, d_cols],
+                                identity=ident_bf[:],
+                            )
+                    copy_out = nc.scalar.copy if first_dt == 0 else nc.vector.tensor_copy
+                    copy_out(out=neg_bf[:, first_dt : first_dt + 2, :], in_=neg_ps[:])
+                    copy_out(out=neg_t[:, first_dt : first_dt + 2, :], in_=neg_ps[:, :, 0:PROD])
+                pos_ps = bank_psum.tile([P, D_TILES, B], BF16, tag="bank")
+                for dt in range(D_TILES):
                     for bt in range(B_TILES):
-                        b_cols = slice(bt * P, (bt + 1) * P)
-                        nc.tensor.matmul_mx(
-                            out=acc[bt][:],
-                            lhsT=vf_codes[:, g, b_cols].bitcast(FP8X4),
-                            lhsT_scale=vf_scales[:, g, b_cols],
-                            rhs=wh_codes[:, g, :].bitcast(FP8X4),
-                            rhs_scale=wh_scales[:, g, :],
-                            start=(c == 0 and g == 0),
-                            stop=(c == CHUNKS - 1 and g == PASSES_PER_CHUNK - 1),
-                        )
-
-            waiting = None
-            codes_before = None
-            for c in range(CHUNKS):
-                rows = load_chunk(c)
-                chunk_codes = new_codes()
-                for g in range(PASSES_PER_CHUNK):
-                    grouped = transpose_pass(rows, g)
-                    if waiting is not None:
-                        quantise_pass(*waiting)
-                    waiting = (grouped, chunk_codes, g)
-                if c > 0:
-                    multiply_chunk(c - 1, codes_before)
-                codes_before = chunk_codes
-            quantise_pass(*waiting)
-
-            neg_sb = keep.tile([P, J_TILES, EMB_D], BF16)
-            nc.sync.dma_start(out=neg_sb[:], in_=n_lfs.rearrange("(jt p) d -> p jt d", p=P))
-            pos_sb = keep.tile([P, B_TILES, EMB_D], BF16)
-            nc.sync.dma_start(out=pos_sb[:], in_=p_lfs.rearrange("(bt p) d -> p bt d", p=P))
-            for first_dt in range(0, D_TILES, 2):
-                neg_ps = bank_psum.tile([P, 2, N_NEG], BF16, tag="bank")
-                for s in range(2):
-                    d_cols = slice((first_dt + s) * P, (first_dt + s + 1) * P)
-                    for jt in range(J_TILES):
                         nc.tensor.transpose(
-                            out=neg_ps[:, s, jt * P : (jt + 1) * P],
-                            in_=neg_sb[:, jt, d_cols],
+                            out=pos_ps[:, dt, bt * P : (bt + 1) * P],
+                            in_=pos_sb[:, bt, dt * P : (dt + 1) * P],
                             identity=ident_bf[:],
                         )
-                copy_out = nc.scalar.copy if first_dt == 0 else nc.vector.tensor_copy
-                copy_out(out=neg_bf[:, first_dt : first_dt + 2, :], in_=neg_ps[:])
-                copy_out(out=neg_t[:, first_dt : first_dt + 2, :], in_=neg_ps[:, :, 0:PROD])
-            pos_ps = bank_psum.tile([P, D_TILES, B], BF16, tag="bank")
-            for dt in range(D_TILES):
-                for bt in range(B_TILES):
-                    nc.tensor.transpose(
-                        out=pos_ps[:, dt, bt * P : (bt + 1) * P],
-                        in_=pos_sb[:, bt, dt * P : (dt + 1) * P],
-                        identity=ident_bf[:],
-                    )
-            nc.scalar.copy(out=pos_t[:], in_=pos_ps[:])
+                nc.scalar.copy(out=pos_t[:], in_=pos_ps[:])
 
-            multiply_chunk(CHUNKS - 1, codes_before)
+
+            waiting = None
+            to_multiply = []
+            first = 0
+            for load_index, count in enumerate(LOADS):
+                rows = load_passes(first, count)
+                if load_index == LABEL_LOAD:
+                    neg_sb = keep.tile([P, J_TILES, EMB_D], BF16)
+                    nc.sync.dma_start(out=neg_sb[:], in_=n_lfs.rearrange("(jt p) d -> p jt d", p=P))
+                    pos_sb = keep.tile([P, B_TILES, EMB_D], BF16)
+                    nc.sync.dma_start(out=pos_sb[:], in_=p_lfs.rearrange("(bt p) d -> p bt d", p=P))
+                if load_index == LABEL_LOAD + 2:
+                    transpose_labels(neg_sb, pos_sb)
+                for g0 in range(0, count, STEP):
+                    for g in range(g0, min(g0 + STEP, count)):
+                        grouped = transpose_pass(rows, g)
+                        if waiting is not None:
+                            quantise_pass(*waiting)
+                        pass_codes = new_codes()
+                        waiting = (grouped, pass_codes)
+                        to_multiply.append((first + g, pass_codes))
+                    while to_multiply and to_multiply[0][0] <= first + g - LAG:
+                        multiply_pass(*to_multiply.pop(0))
+                first += count
+            quantise_pass(*waiting)
+            for n, pass_codes in to_multiply:
+                multiply_pass(n, pass_codes)
 
             hid_sb = [keep.tile([P, HID_D], F32, name="hid_sb%d" % bt) for bt in range(B_TILES)]
             nc.scalar.copy(out=hid_sb[0][:], in_=acc[0][:])
@@ -267,11 +281,12 @@ def tile_hypernymvisual_acc_k_kernel(
                         start=True,
                         stop=True,
                     )
+                add_bias(first_dt, high, emb_ps, H_TILES)
                 add_bias(first_dt, emb_t, emb_ps, H_TILES)
 
         with (
             tc.tile_pool(name="row_maxima", bufs=2 * LEAD + 2) as row_pool,
-            tc.tile_pool(name="col_maxima", bufs=2 * LEAD + 2) as col_pool,
+            tc.tile_pool(name="col_maxima", bufs=4 * LEAD) as col_pool,
             tc.tile_pool(name="scratch", bufs=2) as scratch,
             tc.psum_pool(name="col_psum", bufs=1) as col_psum,
             tc.psum_pool(name="row_psum", bufs=2) as row_psum,
@@ -292,25 +307,15 @@ def tile_hypernymvisual_acc_k_kernel(
                 squares = scratch.tile([P, EMB_D], F32, tag="squares")
                 nc.scalar.activation(out=squares[:], in_=values, func=ACT.Square, accum_out=sum_col)
 
-            parts = keep.tile([P, 2, D_TILES, B], BF16)
-            high = parts[:, 0]
-            high_f32 = keep.tile([P, D_TILES, B], F32)
-            low = keep.tile([P, D_TILES, B], F32)
-            for dt in range(D_TILES):
-                nc.scalar.copy(out=parts[:, 0, dt, :], in_=emb_t[:, dt, :])
-            for dt in range(D_TILES):
-                nc.scalar.copy(out=high_f32[:, dt, :], in_=parts[:, 0, dt, :])
-
-            def split_low():
-                nc.vector.tensor_tensor(out=low[:], in0=emb_t[:], in1=high_f32[:], op=ALU.subtract)
-                nc.scalar.activation(out=parts[:, 1], in_=low[:], func=ACT.Copy, scale=2.0)
+            nc.vector.tensor_copy(out=high_f32[:], in_=high)
+            nc.vector.tensor_tensor(out=parts[:, 1], in0=emb_t[:], in1=high_f32[:], op=ALU.subtract)
 
             row_sums = keep.tile([P, J_TILES, B], F32)
             square_sums = keep.tile([P, 2, B], F32)
-            by_row = keep.tile([P, B_TILES, PROD], F32)
             emb_squares = keep.tile([P, B_TILES], F32)
             pos_sums = keep.tile([P, B_TILES], F32)
-            stats = keep.tile([P, B // VECTOR_PERIOD, 2, STATS], F32)
+            stats = keep.tile([P, len(VECTOR_ROWS), 2, STATS], F32)
+            totals = keep.tile([P, B_TILES, N_NEG], F32)
             col_bank = col_psum.tile([P, B_TILES, PROD], F32, name="col_bank")
 
             def start_by_row():
@@ -327,7 +332,7 @@ def tile_hypernymvisual_acc_k_kernel(
                             stop=(dt == D_TILES - 1),
                         )
                     nc.scalar.activation(
-                        out=by_row[:, bt, :], in_=bank[:, 0:PROD], func=ACT.Identity,
+                        out=totals[:, bt, 0:PROD], in_=bank[:, 0:PROD], func=ACT.Identity,
                         scale=-1.0, bias=emb_squares[:, bt : bt + 1],
                     )
 
@@ -353,78 +358,90 @@ def tile_hypernymvisual_acc_k_kernel(
                     )
                 return maxima
 
-            def turn(maxima, bank):
+            def turn(maxima):
+                bank = turn_psum.tile([P, PER_BANK * P], F32, tag="bank")
                 for dt in range(D_TILES):
                     nc.tensor.transpose(
                         out=bank[:, dt * P : (dt + 1) * P],
                         in_=maxima[:, dt, PROD:].bitcast(F32),
                         identity=ident_f32[:],
                     )
+                return bank
 
-            def wide_pass():
-                bank = turn_psum.tile([P, PER_BANK * P], F32, tag="bank")
+            def four_products(out_cols, maxima, j_cols, weights):
+                for dt in range(D_TILES):
+                    nc.tensor.matmul(
+                        out=out_cols,
+                        lhsT=maxima[:, dt, j_cols],
+                        rhs=weights(dt),
+                        start=(dt == 0),
+                        stop=(dt == D_TILES - 1),
+                    )
+
+            def row_groups(i, maxima, bank):
+                return [
+                    (
+                        bank[:, 0, jt, i % BANK_ROWS, :],
+                        maxima,
+                        slice(jt * P, (jt + 1) * P),
+                        lambda dt: parts[:, :, dt, i],
+                    )
+                    for jt in range(J_TILES)
+                ]
+
+            def column_groups(j, maxima):
+                return [
+                    (
+                        col_bank[:, bt, j : j + 1],
+                        maxima,
+                        slice(bt * P, (bt + 1) * P),
+                        lambda dt: neg_bf[:, dt, j : j + 1],
+                    )
+                    for bt in range(B_TILES)
+                ]
+
+            def wide_pass(row_bank):
                 nc.tensor.matmul_mx(
-                    out=bank[:],
+                    out=row_bank[:, 1].rearrange("p a b c -> p (a b c)"),
                     lhsT=we_codes[:, 0:P].bitcast(FP8X4),
                     lhsT_scale=we_scales[:, 0:P],
-                    rhs=we_codes[:].bitcast(FP8X4),
-                    rhs_scale=we_scales[:],
+                    rhs=we_codes[:, 0:WIDE].bitcast(FP8X4),
+                    rhs_scale=we_scales[:, 0:WIDE],
                     start=True,
                     stop=True,
                 )
-                return bank
-
-            def row_products(i, maxima, bank):
-                for jt in range(J_TILES):
-                    for dt in range(D_TILES):
-                        nc.tensor.matmul(
-                            out=bank[:, jt, i % BANK_ROWS, :],
-                            lhsT=maxima[:, dt, jt * P : (jt + 1) * P],
-                            rhs=parts[:, :, dt, i],
-                            start=(dt == 0),
-                            stop=(dt == D_TILES - 1),
-                        )
-
-            def column_products(j, maxima):
-                for bt in range(B_TILES):
-                    for dt in range(D_TILES):
-                        nc.tensor.matmul(
-                            out=col_bank[:, bt, j : j + 1],
-                            lhsT=maxima[:, dt, bt * P : (bt + 1) * P],
-                            rhs=neg_bf[:, dt, j : j + 1],
-                            start=(dt == 0),
-                            stop=(dt == D_TILES - 1),
-                        )
 
             def sum_squares(i, bank):
                 values = bank[:].bitcast(BF16).rearrange("p (d e) -> p e d", e=2)
                 for e in range(2):
-                    if i % VECTOR_PERIOD == VECTOR_PERIOD - 1:
-                        nc.vector.bn_stats(out=stats[:, i // VECTOR_PERIOD, e, :], in_=values[:, e, :])
+                    if i in VECTOR_ROWS:
+                        nc.vector.bn_stats(
+                            out=stats[:, VECTOR_ROWS.index(i), e, :], in_=values[:, e, :]
+                        )
                     else:
                         scalar_sum_of_squares(values[:, e, :], square_sums[:, e, i : i + 1])
 
             def add_row_products(first_row, bank):
                 i_cols = slice(first_row, first_row + BANK_ROWS)
-                again = scratch.tile([P, J_TILES - PROD_J_TILES, BANK_ROWS], F32, tag="again")
-                nc.scalar.copy(out=again[:], in_=bank[:, PROD_J_TILES:, :, 0])
+                again = scratch.tile([P, PROD_J_TILES, BANK_ROWS], F32, tag="again")
+                nc.scalar.copy(out=again[:], in_=bank[:, 0, 0:PROD_J_TILES, :, 1])
                 nc.vector.tensor_reduce(
-                    out=row_sums[:, :, i_cols], in_=bank[:], axis=mybir.AxisListType.X, op=ALU.add
+                    out=row_sums[:, :, i_cols], in_=bank[:, 0], axis=mybir.AxisListType.X, op=ALU.add
                 )
                 nc.vector.tensor_tensor(
-                    out=row_sums[:, PROD_J_TILES:, i_cols],
-                    in0=row_sums[:, PROD_J_TILES:, i_cols],
+                    out=row_sums[:, 0:PROD_J_TILES, i_cols],
+                    in0=row_sums[:, 0:PROD_J_TILES, i_cols],
                     in1=again[:],
                     op=ALU.add,
                 )
 
             def sums_from_stats():
                 halves = stats[:].rearrange("p i e (h k) -> p i e h k", k=STATS // 2)
-                mean_squares = keep.tile([P, B // VECTOR_PERIOD, 2, 2], F32)
+                mean_squares = keep.tile([P, len(VECTOR_ROWS), 2, 2], F32)
                 nc.vector.tensor_tensor(
                     out=mean_squares[:], in0=halves[:, :, :, :, 1], in1=halves[:, :, :, :, 1], op=ALU.mult
                 )
-                half_sums = keep.tile([P, B // VECTOR_PERIOD, 2, 2], F32)
+                half_sums = keep.tile([P, len(VECTOR_ROWS), 2, 2], F32)
                 nc.vector.scalar_tensor_tensor(
                     out=half_sums[:],
                     in0=mean_squares[:],
@@ -435,15 +452,22 @@ def tile_hypernymvisual_acc_k_kernel(
                 )
                 for e in range(2):
                     nc.vector.tensor_tensor(
-                        out=square_sums[:, e, VECTOR_PERIOD - 1 :: VECTOR_PERIOD],
+                        out=square_sums[:, e, VECTOR_ROWS[0] : B - COL_LEAD : VECTOR_PERIOD],
                         in0=half_sums[:, :, e, 0],
                         in1=half_sums[:, :, e, 1],
                         op=ALU.add,
                     )
 
+            def add_column_products():
+                nc.vector.tensor_tensor(
+                    out=totals[:, :, 0:PROD], in0=totals[:, :, 0:PROD], in1=col_bank[:], op=ALU.add
+                )
+
+            roots = keep.tile([P, B_TILES, 1 + N_NEG], F32)
+            scores = keep.tile([P, B_TILES, 1 + N_NEG], F32)
+
             def finish(bt):
                 i_cols = slice(bt * P, (bt + 1) * P)
-                rows_ps = transpose_four(row_sums, i_cols)
                 squares_ps = turn_psum.tile([P, PER_BANK * P], F32, tag="bank")
                 for e in range(2):
                     nc.tensor.transpose(
@@ -451,60 +475,73 @@ def tile_hypernymvisual_acc_k_kernel(
                         in_=square_sums[:, e, i_cols],
                         identity=ident_f32[:],
                     )
-                totals = scratch.tile([P, N_NEG], F32, tag="totals")
                 nc.scalar.activation(
-                    out=totals[:, PROD:].rearrange("p (w e) -> p w e", e=2),
+                    out=totals[:, bt, PROD:].rearrange("p (w e) -> p w e", e=2),
                     in_=squares_ps[:, 0:SQ].rearrange("p (e w) -> p w e", e=2),
                     func=ACT.Identity,
                     bias=emb_squares[:, bt : bt + 1],
                 )
-                nc.vector.tensor_tensor(
-                    out=totals[:, 0:PROD], in0=by_row[:, bt, :], in1=rows_ps[:, 0:PROD], op=ALU.subtract
+                rows_ps = transpose_four(row_sums, i_cols)
+                nc.scalar.activation(out=roots[:, bt, 0:1], in_=pos_sums[:, bt : bt + 1], func=ACT.Sqrt)
+                for first, end, factor in ((0, PROD, -1.0), (PROD, N_NEG, -2.0)):
+                    half = totals[:, bt, first:end]
+                    nc.vector.scalar_tensor_tensor(
+                        out=half, in0=rows_ps[:, first:end], scalar=factor, in1=half,
+                        op0=ALU.mult, op1=ALU.add,
+                    )
+                for first, end in ((0, PROD), (PROD, N_NEG)):
+                    half = totals[:, bt, first:end]
+                    nc.vector.tensor_scalar_max(out=half, in0=half, scalar1=0.0)
+                    nc.scalar.activation(out=roots[:, bt, 1 + first : 1 + end], in_=half, func=ACT.Sqrt)
+                nc.vector.tensor_scalar_mul(
+                    out=scores[:, bt, 0 : 1 + PROD], in0=roots[:, bt, 0 : 1 + PROD], scalar1=-1.0
                 )
-                nc.vector.tensor_tensor(
-                    out=totals[:, PROD:], in0=totals[:, PROD:], in1=rows_ps[:, PROD:], op=ALU.subtract
+                nc.vector.tensor_scalar_mul(
+                    out=scores[:, bt, 1 + PROD :], in0=roots[:, bt, 1 + PROD :], scalar1=-1.0
                 )
-                nc.vector.tensor_scalar_max(out=totals[:], in0=totals[:], scalar1=0.0)
-                roots = scratch.tile([P, 1 + N_NEG], F32, tag="roots")
-                nc.scalar.activation(out=roots[:, 0:1], in_=pos_sums[:, bt : bt + 1], func=ACT.Sqrt)
-                nc.scalar.activation(out=roots[:, 1:], in_=totals[:], func=ACT.Sqrt)
-                scores = scratch.tile([P, 1 + N_NEG], F32, tag="scores")
-                nc.vector.tensor_scalar_mul(out=scores[:], in0=roots[:], scalar1=-1.0)
-                nc.sync.dma_start(out=out[i_cols, :], in_=scores[:])
+                nc.sync.dma_start(out=out[i_cols, :], in_=scores[:, bt, :])
+
+            def columns_of_step(i):
+                if i < COL_LEAD:
+                    return range(2 * i, 2 * i + 2)
+                return range(i + COL_LEAD, min(i + COL_LEAD + 1, PROD))
 
             made = []
             row_bank = None
-            full_bank = None
+            full_banks = []
             for step in range(0, B + LEAD, RUN):
                 for i in range(step, min(step + RUN, B)):
                     row_maxima = maxima_of(row_pool, neg_bf, high_f32, i)
-                    col_maxima = maxima_of(col_pool, high, neg_t, i)
-                    made.append((row_maxima, col_maxima))
-                if step == 0:
-                    split_low()
-                if full_bank is not None:
-                    add_row_products(*full_bank)
-                    full_bank = None
+                    made.append(
+                        (row_maxima, [(j, maxima_of(col_pool, high, neg_t, j)) for j in columns_of_step(i)])
+                    )
+                if full_banks:
+                    add_row_products(*full_banks.pop())
                 if step >= LEAD:
                     rows = range(step - LEAD, step - LEAD + RUN)
-                    banks = [wide_pass() for i in rows]
-                    for i, bank in zip(rows, banks):
-                        turn(made[i][0], bank)
+                    banks = [turn(made[i][0]) for i in rows]
+                    groups = []
                     for i in rows:
                         if i % BANK_ROWS == 0:
-                            row_bank = row_psum.tile([P, J_TILES, BANK_ROWS, 2], F32, tag="row_bank")
-                        row_products(i, made[i][0], row_bank)
-                        column_products(i, made[i][1])
+                            row_bank = row_psum.tile([P, 2, J_TILES, BANK_ROWS, 2], F32, tag="row_bank")
+                        groups += row_groups(i, made[i][0], row_bank)
+                        for j, col_maxima in made[i][1]:
+                            groups += column_groups(j, col_maxima)
                         if i % BANK_ROWS == BANK_ROWS - 1:
-                            full_bank = (i + 1 - BANK_ROWS, row_bank)
+                            full_banks.append((i + 1 - BANK_ROWS, row_bank))
+                    for n, group in enumerate(groups):
+                        four_products(*group)
+                        if n % WIDE_EVERY == WIDE_EVERY // 2 - 1:
+                            wide_pass(row_bank)
                     for i, bank in zip(rows, banks):
                         sum_squares(i, bank)
                 if step == 8:
                     start_by_row()
                 elif step == 16:
                     positives()
-            add_row_products(*full_bank)
-            sums_from_stats()
-            nc.vector.tensor_tensor(out=by_row[:], in0=by_row[:], in1=col_bank[:], op=ALU.add)
-            for bt in range(B_TILES):
-                finish(bt)
+                elif step == B - 6:
+                    add_column_products()
+                    sums_from_stats()
+                    finish(0)
+            add_row_products(*full_banks.pop())
+            finish(1)

@@ -30,9 +30,7 @@ PROD_J_TILES = PROD // P
 SQ = N_NEG - PROD
 RUN = 2
 LEAD = 4
-BANK_ROWS = 32
-WIDE = 256
-WIDE_EVERY = 4
+BANK_ROWS = 64
 COL_LEAD = 16
 VECTOR_PERIOD = 12
 VECTOR_ROWS = range(VECTOR_PERIOD - 1, B - COL_LEAD, VECTOR_PERIOD)
@@ -64,6 +62,7 @@ def tile_hypernymvisual_acc_k_kernel(
         high_f32 = keep.tile([P, D_TILES, B], F32)
         neg_bf = keep.tile([P, D_TILES, N_NEG], BF16)
         neg_t = keep.tile([P, D_TILES, PROD], F32)
+        neg_squares = keep.tile([P, PROD_J_TILES], F32)
         pos_t = keep.tile([P, D_TILES, B], F32)
 
         with (
@@ -199,6 +198,12 @@ def tile_hypernymvisual_acc_k_kernel(
                             identity=ident_bf[:],
                         )
                 nc.scalar.copy(out=pos_t[:], in_=pos_ps[:])
+                for jt in range(PROD_J_TILES):
+                    squares = work.tile([P, EMB_D], F32, tag="squares")
+                    nc.scalar.activation(
+                        out=squares[:], in_=neg_sb[:, jt, :], func=ACT.Square,
+                        accum_out=neg_squares[:, jt : jt + 1],
+                    )
 
 
             waiting = None
@@ -318,22 +323,10 @@ def tile_hypernymvisual_acc_k_kernel(
             totals = keep.tile([P, B_TILES, N_NEG], F32)
             col_bank = col_psum.tile([P, B_TILES, PROD], F32, name="col_bank")
 
-            def start_by_row():
+            def sum_emb_squares():
                 for bt in range(B_TILES):
-                    i_cols = slice(bt * P, (bt + 1) * P)
-                    scalar_sum_of_squares(transpose_four(emb_t, i_cols)[:], emb_squares[:, bt : bt + 1])
-                    bank = turn_psum.tile([P, PER_BANK * P], F32, tag="bank")
-                    for dt in range(D_TILES):
-                        nc.tensor.matmul(
-                            out=bank[:, 0:PROD],
-                            lhsT=parts[:, 0, dt, i_cols],
-                            rhs=neg_bf[:, dt, 0:PROD],
-                            start=(dt == 0),
-                            stop=(dt == D_TILES - 1),
-                        )
-                    nc.scalar.activation(
-                        out=totals[:, bt, 0:PROD], in_=bank[:, 0:PROD], func=ACT.Identity,
-                        scale=-1.0, bias=emb_squares[:, bt : bt + 1],
+                    scalar_sum_of_squares(
+                        transpose_four(emb_t, slice(bt * P, (bt + 1) * P))[:], emb_squares[:, bt : bt + 1]
                     )
 
             def positives():
@@ -346,33 +339,31 @@ def tile_hypernymvisual_acc_k_kernel(
                         pos_sums[:, bt : bt + 1],
                     )
 
-            def maxima_of(pool, source, scalars, index):
-                maxima = pool.tile([P, D_TILES, source.shape[2]], BF16, tag="maxima")
+            def against(op, pool, source, scalars, index):
+                result = pool.tile([P, D_TILES, source.shape[2]], BF16, tag="result")
                 for dt in range(D_TILES):
                     nc.vector.tensor_scalar(
-                        out=maxima[:, dt, :],
+                        out=result[:, dt, :],
                         in0=source[:, dt, :],
                         scalar1=scalars[:, dt, index : index + 1],
                         scalar2=None,
-                        op0=ALU.max,
+                        op0=op,
                     )
-                return maxima
+                return result
 
-            def turn(maxima):
-                bank = turn_psum.tile([P, PER_BANK * P], F32, tag="bank")
+            def turn(maxima, bank):
                 for dt in range(D_TILES):
                     nc.tensor.transpose(
                         out=bank[:, dt * P : (dt + 1) * P],
                         in_=maxima[:, dt, PROD:].bitcast(F32),
                         identity=ident_f32[:],
                     )
-                return bank
 
-            def four_products(out_cols, maxima, j_cols, weights):
+            def four_products(out_cols, values, cols, weights):
                 for dt in range(D_TILES):
                     nc.tensor.matmul(
                         out=out_cols,
-                        lhsT=maxima[:, dt, j_cols],
+                        lhsT=values[:, dt, cols],
                         rhs=weights(dt),
                         start=(dt == 0),
                         stop=(dt == D_TILES - 1),
@@ -381,7 +372,7 @@ def tile_hypernymvisual_acc_k_kernel(
             def row_groups(i, maxima, bank):
                 return [
                     (
-                        bank[:, 0, jt, i % BANK_ROWS, :],
+                        bank[:, jt, i % BANK_ROWS, :],
                         maxima,
                         slice(jt * P, (jt + 1) * P),
                         lambda dt: parts[:, :, dt, i],
@@ -389,27 +380,29 @@ def tile_hypernymvisual_acc_k_kernel(
                     for jt in range(J_TILES)
                 ]
 
-            def column_groups(j, maxima):
+            def column_groups(j, minima):
                 return [
                     (
                         col_bank[:, bt, j : j + 1],
-                        maxima,
+                        minima,
                         slice(bt * P, (bt + 1) * P),
                         lambda dt: neg_bf[:, dt, j : j + 1],
                     )
                     for bt in range(B_TILES)
                 ]
 
-            def wide_pass(row_bank):
+            def wide_pass():
+                bank = turn_psum.tile([P, PER_BANK * P], F32, tag="bank")
                 nc.tensor.matmul_mx(
-                    out=row_bank[:, 1].rearrange("p a b c -> p (a b c)"),
+                    out=bank[:],
                     lhsT=we_codes[:, 0:P].bitcast(FP8X4),
                     lhsT_scale=we_scales[:, 0:P],
-                    rhs=we_codes[:, 0:WIDE].bitcast(FP8X4),
-                    rhs_scale=we_scales[:, 0:WIDE],
+                    rhs=we_codes[:].bitcast(FP8X4),
+                    rhs_scale=we_scales[:],
                     start=True,
                     stop=True,
                 )
+                return bank
 
             def sum_squares(i, bank):
                 values = bank[:].bitcast(BF16).rearrange("p (d e) -> p e d", e=2)
@@ -424,16 +417,19 @@ def tile_hypernymvisual_acc_k_kernel(
             def add_row_products(first_row, bank):
                 i_cols = slice(first_row, first_row + BANK_ROWS)
                 again = scratch.tile([P, PROD_J_TILES, BANK_ROWS], F32, tag="again")
-                nc.scalar.copy(out=again[:], in_=bank[:, 0, 0:PROD_J_TILES, :, 1])
+                nc.scalar.copy(out=again[:], in_=bank[:, 0:PROD_J_TILES, :, 1])
                 nc.vector.tensor_reduce(
-                    out=row_sums[:, :, i_cols], in_=bank[:, 0], axis=mybir.AxisListType.X, op=ALU.add
+                    out=row_sums[:, :, i_cols], in_=bank[:], axis=mybir.AxisListType.X, op=ALU.add
                 )
-                nc.vector.tensor_tensor(
-                    out=row_sums[:, 0:PROD_J_TILES, i_cols],
-                    in0=row_sums[:, 0:PROD_J_TILES, i_cols],
-                    in1=again[:],
-                    op=ALU.add,
-                )
+                for jt in range(PROD_J_TILES):
+                    nc.vector.scalar_tensor_tensor(
+                        out=row_sums[:, jt, i_cols],
+                        in0=row_sums[:, jt, i_cols],
+                        scalar=neg_squares[:, jt : jt + 1],
+                        in1=again[:, jt, :],
+                        op0=ALU.subtract,
+                        op1=ALU.add,
+                    )
 
             def sums_from_stats():
                 halves = stats[:].rearrange("p i e (h k) -> p i e h k", k=STATS // 2)
@@ -458,10 +454,12 @@ def tile_hypernymvisual_acc_k_kernel(
                         op=ALU.add,
                     )
 
-            def add_column_products():
-                nc.vector.tensor_tensor(
-                    out=totals[:, :, 0:PROD], in0=totals[:, :, 0:PROD], in1=col_bank[:], op=ALU.add
-                )
+            def take_column_products():
+                for bt in range(B_TILES):
+                    nc.scalar.activation(
+                        out=totals[:, bt, 0:PROD], in_=col_bank[:, bt, :], func=ACT.Identity,
+                        scale=-1.0, bias=emb_squares[:, bt : bt + 1],
+                    )
 
             roots = keep.tile([P, B_TILES, 1 + N_NEG], F32)
             scores = keep.tile([P, B_TILES, 1 + N_NEG], F32)
@@ -511,36 +509,37 @@ def tile_hypernymvisual_acc_k_kernel(
             full_banks = []
             for step in range(0, B + LEAD, RUN):
                 for i in range(step, min(step + RUN, B)):
-                    row_maxima = maxima_of(row_pool, neg_bf, high_f32, i)
-                    made.append(
-                        (row_maxima, [(j, maxima_of(col_pool, high, neg_t, j)) for j in columns_of_step(i)])
-                    )
+                    maxima = against(ALU.max, row_pool, neg_bf, high_f32, i)
+                    minima = [
+                        (j, against(ALU.min, col_pool, high, neg_t, j)) for j in columns_of_step(i)
+                    ]
+                    made.append((maxima, minima))
                 if full_banks:
                     add_row_products(*full_banks.pop())
                 if step >= LEAD:
                     rows = range(step - LEAD, step - LEAD + RUN)
-                    banks = [turn(made[i][0]) for i in rows]
+                    banks = [wide_pass() for i in rows]
+                    for i, bank in zip(rows, banks):
+                        turn(made[i][0], bank)
                     groups = []
                     for i in rows:
                         if i % BANK_ROWS == 0:
-                            row_bank = row_psum.tile([P, 2, J_TILES, BANK_ROWS, 2], F32, tag="row_bank")
+                            row_bank = row_psum.tile([P, J_TILES, BANK_ROWS, 2], F32, tag="row_bank")
                         groups += row_groups(i, made[i][0], row_bank)
-                        for j, col_maxima in made[i][1]:
-                            groups += column_groups(j, col_maxima)
+                        for j, minima in made[i][1]:
+                            groups += column_groups(j, minima)
                         if i % BANK_ROWS == BANK_ROWS - 1:
                             full_banks.append((i + 1 - BANK_ROWS, row_bank))
-                    for n, group in enumerate(groups):
+                    for group in groups:
                         four_products(*group)
-                        if n % WIDE_EVERY == WIDE_EVERY // 2 - 1:
-                            wide_pass(row_bank)
                     for i, bank in zip(rows, banks):
                         sum_squares(i, bank)
                 if step == 8:
-                    start_by_row()
+                    sum_emb_squares()
                 elif step == 16:
                     positives()
                 elif step == B - 6:
-                    add_column_products()
+                    take_column_products()
                     sums_from_stats()
                     finish(0)
             add_row_products(*full_banks.pop())

@@ -15,9 +15,8 @@ P = 128
 QUAD = 4
 K_PASS = P * QUAD
 PASSES = VF_D // K_PASS
-LOADS = [1, 1, 2] + [4] * 6 + [2, 1, 1]
+LOADS = [1, 1, 2] + [4] * 7
 MOST_PASSES = max(LOADS)
-LABEL_LOAD = 3
 STEP = 4
 LAG = 2
 B_TILES = B // P
@@ -31,9 +30,9 @@ SQ = N_NEG - PROD
 RUN = 2
 LEAD = 4
 BANK_ROWS = 64
-COL_LEAD = 16
+WIDE = [512, 256]
 VECTOR_PERIOD = 12
-VECTOR_ROWS = range(VECTOR_PERIOD - 1, B - COL_LEAD, VECTOR_PERIOD)
+VECTOR_ROWS = range(VECTOR_PERIOD - 1, B - 16, VECTOR_PERIOD)
 STATS = 6
 PSUM_BANKS = 8
 PER_BANK = 4
@@ -198,26 +197,13 @@ def tile_hypernymvisual_acc_k_kernel(
                             identity=ident_bf[:],
                         )
                 nc.scalar.copy(out=pos_t[:], in_=pos_ps[:])
-                for jt in range(PROD_J_TILES):
-                    squares = work.tile([P, EMB_D], F32, tag="squares")
-                    nc.scalar.activation(
-                        out=squares[:], in_=neg_sb[:, jt, :], func=ACT.Square,
-                        accum_out=neg_squares[:, jt : jt + 1],
-                    )
 
 
             waiting = None
             to_multiply = []
             first = 0
-            for load_index, count in enumerate(LOADS):
+            for count in LOADS:
                 rows = load_passes(first, count)
-                if load_index == LABEL_LOAD:
-                    neg_sb = keep.tile([P, J_TILES, EMB_D], BF16)
-                    nc.sync.dma_start(out=neg_sb[:], in_=n_lfs.rearrange("(jt p) d -> p jt d", p=P))
-                    pos_sb = keep.tile([P, B_TILES, EMB_D], BF16)
-                    nc.sync.dma_start(out=pos_sb[:], in_=p_lfs.rearrange("(bt p) d -> p bt d", p=P))
-                if load_index == LABEL_LOAD + 2:
-                    transpose_labels(neg_sb, pos_sb)
                 for g0 in range(0, count, STEP):
                     for g in range(g0, min(g0 + STEP, count)):
                         grouped = transpose_pass(rows, g)
@@ -230,6 +216,11 @@ def tile_hypernymvisual_acc_k_kernel(
                         multiply_pass(*to_multiply.pop(0))
                 first += count
             quantise_pass(*waiting)
+            neg_sb = keep.tile([P, J_TILES, EMB_D], BF16)
+            nc.sync.dma_start(out=neg_sb[:], in_=n_lfs.rearrange("(jt p) d -> p jt d", p=P))
+            pos_sb = keep.tile([P, B_TILES, EMB_D], BF16)
+            nc.sync.dma_start(out=pos_sb[:], in_=p_lfs.rearrange("(bt p) d -> p bt d", p=P))
+            transpose_labels(neg_sb, pos_sb)
             for n, pass_codes in to_multiply:
                 multiply_pass(n, pass_codes)
 
@@ -273,8 +264,9 @@ def tile_hypernymvisual_acc_k_kernel(
                 in_=hid_grouped[:].rearrange("p b t -> p (b t)"),
             )
 
+            emb_banks = []
             for first_dt in range(0, D_TILES, 2):
-                emb_ps = bank_psum.tile([P, 2, B], F32, tag="bank")
+                emb_ps = acc_psum.tile([P, 2, B], F32, name="acc%d" % (first_dt // 2))
                 for s in range(2):
                     d_cols = slice((first_dt + s) * P, (first_dt + s + 1) * P)
                     nc.tensor.matmul_mx(
@@ -287,11 +279,29 @@ def tile_hypernymvisual_acc_k_kernel(
                         stop=True,
                     )
                 add_bias(first_dt, high, emb_ps, H_TILES)
-                add_bias(first_dt, emb_t, emb_ps, H_TILES)
+                emb_banks.append(emb_ps)
+            nc.scalar.copy(out=high_f32[:, 0:2, :], in_=high[:, 0:2, :])
+            nc.vector.tensor_copy(out=high_f32[:, 2:4, :], in_=high[:, 2:4, :])
+            for dt in (2, 3, 0, 1):
+                nc.vector.scalar_tensor_tensor(
+                    out=parts[:, 1, dt, :],
+                    in0=emb_banks[dt // 2][:, dt % 2, :],
+                    scalar=bias_cols[:, H_TILES + dt : H_TILES + dt + 1],
+                    in1=high_f32[:, dt, :],
+                    op0=ALU.add,
+                    op1=ALU.subtract,
+                )
+            for dt in range(D_TILES):
+                nc.scalar.activation(
+                    out=emb_t[:, dt, :],
+                    in_=emb_banks[dt // 2][:, dt % 2, :],
+                    func=ACT.Identity,
+                    bias=bias_cols[:, H_TILES + dt : H_TILES + dt + 1],
+                )
 
         with (
             tc.tile_pool(name="row_maxima", bufs=2 * LEAD + 2) as row_pool,
-            tc.tile_pool(name="col_maxima", bufs=4 * LEAD) as col_pool,
+            tc.tile_pool(name="col_maxima", bufs=2 * LEAD + 2) as col_pool,
             tc.tile_pool(name="scratch", bufs=2) as scratch,
             tc.psum_pool(name="col_psum", bufs=1) as col_psum,
             tc.psum_pool(name="row_psum", bufs=2) as row_psum,
@@ -312,9 +322,6 @@ def tile_hypernymvisual_acc_k_kernel(
                 squares = scratch.tile([P, EMB_D], F32, tag="squares")
                 nc.scalar.activation(out=squares[:], in_=values, func=ACT.Square, accum_out=sum_col)
 
-            nc.vector.tensor_copy(out=high_f32[:], in_=high)
-            nc.vector.tensor_tensor(out=parts[:, 1], in0=emb_t[:], in1=high_f32[:], op=ALU.subtract)
-
             row_sums = keep.tile([P, J_TILES, B], F32)
             square_sums = keep.tile([P, 2, B], F32)
             emb_squares = keep.tile([P, B_TILES], F32)
@@ -323,7 +330,9 @@ def tile_hypernymvisual_acc_k_kernel(
             totals = keep.tile([P, B_TILES, N_NEG], F32)
             col_bank = col_psum.tile([P, B_TILES, PROD], F32, name="col_bank")
 
-            def sum_emb_squares():
+            def sum_own_squares():
+                for jt in range(PROD_J_TILES):
+                    scalar_sum_of_squares(neg_sb[:, jt, :], neg_squares[:, jt : jt + 1])
                 for bt in range(B_TILES):
                     scalar_sum_of_squares(
                         transpose_four(emb_t, slice(bt * P, (bt + 1) * P))[:], emb_squares[:, bt : bt + 1]
@@ -391,14 +400,14 @@ def tile_hypernymvisual_acc_k_kernel(
                     for bt in range(B_TILES)
                 ]
 
-            def wide_pass():
+            def wide_pass(columns):
                 bank = turn_psum.tile([P, PER_BANK * P], F32, tag="bank")
                 nc.tensor.matmul_mx(
-                    out=bank[:],
+                    out=bank[:, 0:columns],
                     lhsT=we_codes[:, 0:P].bitcast(FP8X4),
                     lhsT_scale=we_scales[:, 0:P],
-                    rhs=we_codes[:].bitcast(FP8X4),
-                    rhs_scale=we_scales[:],
+                    rhs=we_codes[:, 0:columns].bitcast(FP8X4),
+                    rhs_scale=we_scales[:, 0:columns],
                     start=True,
                     stop=True,
                 )
@@ -416,8 +425,6 @@ def tile_hypernymvisual_acc_k_kernel(
 
             def add_row_products(first_row, bank):
                 i_cols = slice(first_row, first_row + BANK_ROWS)
-                again = scratch.tile([P, PROD_J_TILES, BANK_ROWS], F32, tag="again")
-                nc.scalar.copy(out=again[:], in_=bank[:, 0:PROD_J_TILES, :, 1])
                 nc.vector.tensor_reduce(
                     out=row_sums[:, :, i_cols], in_=bank[:], axis=mybir.AxisListType.X, op=ALU.add
                 )
@@ -426,18 +433,21 @@ def tile_hypernymvisual_acc_k_kernel(
                         out=row_sums[:, jt, i_cols],
                         in0=row_sums[:, jt, i_cols],
                         scalar=neg_squares[:, jt : jt + 1],
-                        in1=again[:, jt, :],
+                        in1=bank[:, jt, :, 1],
                         op0=ALU.subtract,
                         op1=ALU.add,
                     )
 
-            def sums_from_stats():
-                halves = stats[:].rearrange("p i e (h k) -> p i e h k", k=STATS // 2)
-                mean_squares = keep.tile([P, len(VECTOR_ROWS), 2, 2], F32)
+            def sums_from_stats(bt):
+                count = len(VECTOR_ROWS) // B_TILES
+                halves = stats[:, bt * count : (bt + 1) * count].rearrange(
+                    "p i e (h k) -> p i e h k", k=STATS // 2
+                )
+                mean_squares = scratch.tile([P, count, 2, 2], F32, tag="mean_squares")
                 nc.vector.tensor_tensor(
                     out=mean_squares[:], in0=halves[:, :, :, :, 1], in1=halves[:, :, :, :, 1], op=ALU.mult
                 )
-                half_sums = keep.tile([P, len(VECTOR_ROWS), 2, 2], F32)
+                half_sums = scratch.tile([P, count, 2, 2], F32, tag="half_sums")
                 nc.vector.scalar_tensor_tensor(
                     out=half_sums[:],
                     in0=mean_squares[:],
@@ -446,25 +456,29 @@ def tile_hypernymvisual_acc_k_kernel(
                     op0=ALU.mult,
                     op1=ALU.add,
                 )
+                first = VECTOR_ROWS[bt * count]
                 for e in range(2):
                     nc.vector.tensor_tensor(
-                        out=square_sums[:, e, VECTOR_ROWS[0] : B - COL_LEAD : VECTOR_PERIOD],
+                        out=square_sums[:, e, first : first + count * VECTOR_PERIOD : VECTOR_PERIOD],
                         in0=half_sums[:, :, e, 0],
                         in1=half_sums[:, :, e, 1],
                         op=ALU.add,
                     )
 
-            def take_column_products():
-                for bt in range(B_TILES):
-                    nc.scalar.activation(
-                        out=totals[:, bt, 0:PROD], in_=col_bank[:, bt, :], func=ACT.Identity,
-                        scale=-1.0, bias=emb_squares[:, bt : bt + 1],
-                    )
-
             roots = keep.tile([P, B_TILES, 1 + N_NEG], F32)
             scores = keep.tile([P, B_TILES, 1 + N_NEG], F32)
 
-            def finish(bt):
+            def take_root(bt, first, end):
+                half = totals[:, bt, first:end]
+                nc.vector.tensor_scalar_max(out=half, in0=half, scalar1=0.0)
+                nc.scalar.activation(out=roots[:, bt, 1 + first : 1 + end], in_=half, func=ACT.Sqrt)
+                nc.vector.tensor_scalar_mul(
+                    out=scores[:, bt, 1 + first : 1 + end],
+                    in0=roots[:, bt, 1 + first : 1 + end],
+                    scalar1=-1.0,
+                )
+
+            def finish_squares(bt):
                 i_cols = slice(bt * P, (bt + 1) * P)
                 squares_ps = turn_psum.tile([P, PER_BANK * P], F32, tag="bank")
                 for e in range(2):
@@ -480,45 +494,41 @@ def tile_hypernymvisual_acc_k_kernel(
                     bias=emb_squares[:, bt : bt + 1],
                 )
                 rows_ps = transpose_four(row_sums, i_cols)
+                nc.scalar.activation(
+                    out=totals[:, bt, 0:PROD], in_=rows_ps[:, 0:PROD], func=ACT.Identity,
+                    scale=-1.0, bias=emb_squares[:, bt : bt + 1],
+                )
+                nc.vector.scalar_tensor_tensor(
+                    out=totals[:, bt, PROD:], in0=rows_ps[:, PROD:], scalar=-2.0,
+                    in1=totals[:, bt, PROD:], op0=ALU.mult, op1=ALU.add,
+                )
                 nc.scalar.activation(out=roots[:, bt, 0:1], in_=pos_sums[:, bt : bt + 1], func=ACT.Sqrt)
-                for first, end, factor in ((0, PROD, -1.0), (PROD, N_NEG, -2.0)):
-                    half = totals[:, bt, first:end]
-                    nc.vector.scalar_tensor_tensor(
-                        out=half, in0=rows_ps[:, first:end], scalar=factor, in1=half,
-                        op0=ALU.mult, op1=ALU.add,
-                    )
-                for first, end in ((0, PROD), (PROD, N_NEG)):
-                    half = totals[:, bt, first:end]
-                    nc.vector.tensor_scalar_max(out=half, in0=half, scalar1=0.0)
-                    nc.scalar.activation(out=roots[:, bt, 1 + first : 1 + end], in_=half, func=ACT.Sqrt)
-                nc.vector.tensor_scalar_mul(
-                    out=scores[:, bt, 0 : 1 + PROD], in0=roots[:, bt, 0 : 1 + PROD], scalar1=-1.0
-                )
-                nc.vector.tensor_scalar_mul(
-                    out=scores[:, bt, 1 + PROD :], in0=roots[:, bt, 1 + PROD :], scalar1=-1.0
-                )
-                nc.sync.dma_start(out=out[i_cols, :], in_=scores[:, bt, :])
+                nc.vector.tensor_scalar_mul(out=scores[:, bt, 0:1], in0=roots[:, bt, 0:1], scalar1=-1.0)
+                take_root(bt, PROD, N_NEG)
 
-            def columns_of_step(i):
-                if i < COL_LEAD:
-                    return range(2 * i, 2 * i + 2)
-                return range(i + COL_LEAD, min(i + COL_LEAD + 1, PROD))
+            def finish_products(bt):
+                nc.vector.scalar_tensor_tensor(
+                    out=totals[:, bt, 0:PROD], in0=col_bank[:, bt, :], scalar=-1.0,
+                    in1=totals[:, bt, 0:PROD], op0=ALU.mult, op1=ALU.add,
+                )
+                take_root(bt, 0, PROD)
+                nc.sync.dma_start(out=out[bt * P : (bt + 1) * P, :], in_=scores[:, bt, :])
 
+            for columns in WIDE + WIDE:
+                wide_pass(columns)
             made = []
             row_bank = None
             full_banks = []
             for step in range(0, B + LEAD, RUN):
                 for i in range(step, min(step + RUN, B)):
                     maxima = against(ALU.max, row_pool, neg_bf, high_f32, i)
-                    minima = [
-                        (j, against(ALU.min, col_pool, high, neg_t, j)) for j in columns_of_step(i)
-                    ]
+                    minima = against(ALU.min, col_pool, high, neg_t, i)
                     made.append((maxima, minima))
                 if full_banks:
                     add_row_products(*full_banks.pop())
                 if step >= LEAD:
                     rows = range(step - LEAD, step - LEAD + RUN)
-                    banks = [wide_pass() for i in rows]
+                    banks = [wide_pass(columns) for columns in WIDE]
                     for i, bank in zip(rows, banks):
                         turn(made[i][0], bank)
                     groups = []
@@ -526,8 +536,7 @@ def tile_hypernymvisual_acc_k_kernel(
                         if i % BANK_ROWS == 0:
                             row_bank = row_psum.tile([P, J_TILES, BANK_ROWS, 2], F32, tag="row_bank")
                         groups += row_groups(i, made[i][0], row_bank)
-                        for j, minima in made[i][1]:
-                            groups += column_groups(j, minima)
+                        groups += column_groups(i, made[i][1])
                         if i % BANK_ROWS == BANK_ROWS - 1:
                             full_banks.append((i + 1 - BANK_ROWS, row_bank))
                     for group in groups:
@@ -535,12 +544,15 @@ def tile_hypernymvisual_acc_k_kernel(
                     for i, bank in zip(rows, banks):
                         sum_squares(i, bank)
                 if step == 8:
-                    sum_emb_squares()
+                    sum_own_squares()
                 elif step == 16:
                     positives()
-                elif step == B - 6:
-                    take_column_products()
-                    sums_from_stats()
-                    finish(0)
+                elif step == P + 10:
+                    sums_from_stats(0)
+                    finish_squares(0)
+                elif step == B - 4:
+                    sums_from_stats(1)
             add_row_products(*full_banks.pop())
-            finish(1)
+            finish_products(0)
+            finish_squares(1)
+            finish_products(1)

import concourse.mybir as mybir
from concourse.masks import make_identity

F32 = mybir.dt.float32
BF16 = mybir.dt.bfloat16
U32 = mybir.dt.uint32
U8 = mybir.dt.uint8
FP8X4 = mybir.dt.float8_e4m3fn_x4
ALU = mybir.AluOpType
ACT = mybir.ActivationFunctionType

B, N_NEG, VF_D, HID_D, EMB_D = 256, 512, 16384, 512, 512

P = 128
QUAD = 4
K_PASS = P * QUAD
PASSES = VF_D // K_PASS
LOADS = [1, 1, 2] + [4] * 7
MOST_PASSES = max(LOADS)
STEP = 4
LAG = 2
B_TILES = B // P
H_TILES = HID_D // P
ROW_TILES = B_TILES + H_TILES
D_TILES = EMB_D // P
J_TILES = N_NEG // P
PROD = N_NEG // 2
PROD_J_TILES = PROD // P
SQ = N_NEG - PROD
RUN = 2
LEAD = 4
BANK_ROWS = 64
WIDE = [512, 256]
VECTOR_PERIOD = 12
VECTOR_ROWS = range(VECTOR_PERIOD - 1, B - 16, VECTOR_PERIOD)
STATS = 6
PSUM_BANKS = 8
PER_BANK = 4

FLOPS = 2 * B * VF_D * HID_D + 2 * B * HID_D * EMB_D


def tile_hypernymvisual_acc_k_kernel(
    tc, vfs, p_lfs, n_lfs, W_hidden, b_hidden, W_embed, b_embed, out
):
    nc = tc.nc
    with tc.manual_schedule(), tc.tile_pool(name="keep", bufs=1) as keep:
        ident_bf = keep.tile([P, P], BF16)
        make_identity(nc, ident_bf[:])
        ident_f32 = keep.tile([P, P], F32)
        make_identity(nc, ident_f32[:])

        one = keep.tile([P, 1], F32)
        nc.vector.memset(one[:], 1.0)
        one_root = keep.tile([P, 1], F32)
        nc.scalar.activation(out=one_root[:], in_=one[:], func=ACT.Sqrt)

        emb_t = keep.tile([P, D_TILES, B], F32)
        parts = keep.tile([P, 2, D_TILES, B], BF16)
        high = parts[:, 0]
        high_f32 = keep.tile([P, D_TILES, B], F32)
        neg_bf = keep.tile([P, D_TILES, N_NEG], BF16)
        neg_t = keep.tile([P, D_TILES, PROD], F32)
        neg_squares = keep.tile([P, PROD_J_TILES], F32)
        pos_t = keep.tile([P, D_TILES, B], F32)

        with (
            tc.tile_pool(name="load", bufs=4) as load,
            tc.tile_pool(name="work", bufs=3) as work,
            tc.tile_pool(name="codes", bufs=STEP + LAG + 2) as codes,
            tc.psum_pool(name="acc_psum", bufs=1) as acc_psum,
            tc.psum_pool(name="bank_psum", bufs=PSUM_BANKS - B_TILES) as bank_psum,
        ):
            bias_rows = keep.tile([P, P], BF16)
            nc.vector.memset(bias_rows[:], 0.0)
            nc.sync.dma_start(
                out=bias_rows[0:H_TILES, :], in_=b_hidden.rearrange("(t p) -> t p", p=P)
            )
            nc.sync.dma_start(
                out=bias_rows[H_TILES : H_TILES + D_TILES, :],
                in_=b_embed.rearrange("(t p) -> t p", p=P),
            )
            bias_ps = bank_psum.tile([P, P], BF16, tag="bank")
            nc.tensor.transpose(out=bias_ps[:], in_=bias_rows[:], identity=ident_bf[:])
            bias_cols = keep.tile([P, H_TILES + D_TILES], F32)
            nc.vector.tensor_copy(out=bias_cols[:], in_=bias_ps[:, 0 : H_TILES + D_TILES])

            we_sb = keep.tile([P, D_TILES, HID_D], BF16)
            nc.sync.dma_start(out=we_sb[:], in_=W_embed.rearrange("(dt p) h -> p dt h", p=P))
            we_grouped = keep.tile([P, EMB_D, QUAD], BF16, align_bytes=64)
            for dt in range(D_TILES):
                we_ps = bank_psum.tile([P, QUAD, P], BF16, tag="bank")
                for t in range(QUAD):
                    nc.tensor.transpose(
                        out=we_ps[:, t, :],
                        in_=we_sb[:, dt, t * P : (t + 1) * P],
                        identity=ident_bf[:],
                    )
                nc.vector.tensor_copy(
                    out=we_grouped[:, dt * P : (dt + 1) * P, :],
                    in_=we_ps[:].rearrange("p t r -> p r t"),
                )
            we_codes = keep.tile([P, EMB_D], U32, align_bytes=64)
            we_scales = keep.tile([P, EMB_D], U8, align_bytes=64)
            nc.vector.quantize_mx(
                out=we_codes[:].bitcast(FP8X4),
                scales=we_scales[:],
                in_=we_grouped[:].rearrange("p r t -> p (r t)"),
            )

            vf_view = vfs.rearrange("(t p) k -> p t k", p=P)
            wh_view = W_hidden.rearrange("(t p) k -> p t k", p=P)
            acc = [acc_psum.tile([P, HID_D], F32, name="acc%d" % bt) for bt in range(B_TILES)]

            def load_passes(first, count):
                rows = load.tile([P, ROW_TILES, MOST_PASSES * K_PASS], BF16, tag="rows")
                width = count * K_PASS
                k_cols = slice(first * K_PASS, first * K_PASS + width)
                nc.sync.dma_start(out=rows[:, 0:B_TILES, 0:width], in_=vf_view[:, :, k_cols])
                nc.sync.dma_start(out=rows[:, B_TILES:ROW_TILES, 0:width], in_=wh_view[:, :, k_cols])
                return rows

            def transpose_pass(rows, g):
                rows_f32 = rows[:].bitcast(F32)
                grouped = work.tile([P, ROW_TILES * P * QUAD], BF16, tag="grouped", align_bytes=64)
                grouped_f32 = grouped[:].bitcast(F32).rearrange(
                    "p (t r u) -> p t r u", t=ROW_TILES, u=2
                )
                for first_tile in range(0, ROW_TILES, 2):
                    bank = bank_psum.tile([P, 2, 2, P], F32, tag="bank")
                    for s in range(2):
                        for u in range(2):
                            col = g * (K_PASS // 2) + u * P
                            nc.tensor.transpose(
                                out=bank[:, s, u, :],
                                in_=rows_f32[:, first_tile + s, col : col + P],
                                identity=ident_f32[:],
                            )
                    copy_out = nc.scalar.copy if first_tile + 2 < ROW_TILES else nc.vector.tensor_copy
                    copy_out(
                        out=grouped_f32[:, first_tile : first_tile + 2, :, :],
                        in_=bank[:].rearrange("p s u r -> p s r u"),
                    )
                return grouped

            def new_codes():
                vf_codes = codes.tile([P, B], U32, tag="vf_codes", align_bytes=64)
                vf_scales = codes.tile([P, B], U8, tag="vf_scales", align_bytes=64)
                wh_codes = codes.tile([P, HID_D], U32, tag="wh_codes", align_bytes=64)
                wh_scales = codes.tile([P, HID_D], U8, tag="wh_scales", align_bytes=64)
                return vf_codes, vf_scales, wh_codes, wh_scales

            def quantise_pass(grouped, pass_codes):
                vf_codes, vf_scales, wh_codes, wh_scales = pass_codes
                vf_end = B * QUAD
                nc.vector.quantize_mx(
                    out=vf_codes[:].bitcast(FP8X4), scales=vf_scales[:], in_=grouped[:, 0:vf_end]
                )
                nc.vector.quantize_mx(
                    out=wh_codes[:].bitcast(FP8X4), scales=wh_scales[:], in_=grouped[:, vf_end:]
                )

            def multiply_pass(n, pass_codes):
                vf_codes, vf_scales, wh_codes, wh_scales = pass_codes
                for bt in range(B_TILES):
                    b_cols = slice(bt * P, (bt + 1) * P)
                    nc.tensor.matmul_mx(
                        out=acc[bt][:],
                        lhsT=vf_codes[:, b_cols].bitcast(FP8X4),
                        lhsT_scale=vf_scales[:, b_cols],
                        rhs=wh_codes[:].bitcast(FP8X4),
                        rhs_scale=wh_scales[:],
                        start=(n == 0),
                        stop=(n == PASSES - 1),
                    )

            def transpose_labels(neg_sb, pos_sb):
                for first_dt in range(0, D_TILES, 2):
                    neg_ps = bank_psum.tile([P, 2, N_NEG], BF16, tag="bank")
                    for s in range(2):
                        d_cols = slice((first_dt + s) * P, (first_dt + s + 1) * P)
                        for jt in range(J_TILES):
                            nc.tensor.transpose(
                                out=neg_ps[:, s, jt * P : (jt + 1) * P],
                                in_=neg_sb[:, jt, d_cols],
                                identity=ident_bf[:],
                            )
                    copy_out = nc.scalar.copy if first_dt == 0 else nc.vector.tensor_copy
                    copy_out(out=neg_bf[:, first_dt : first_dt + 2, :], in_=neg_ps[:])
                    copy_out(out=neg_t[:, first_dt : first_dt + 2, :], in_=neg_ps[:, :, 0:PROD])
                pos_ps = bank_psum.tile([P, D_TILES, B], BF16, tag="bank")
                for dt in range(D_TILES):
                    for bt in range(B_TILES):
                        nc.tensor.transpose(
                            out=pos_ps[:, dt, bt * P : (bt + 1) * P],
                            in_=pos_sb[:, bt, dt * P : (dt + 1) * P],
                            identity=ident_bf[:],
                        )
                nc.scalar.copy(out=pos_t[:], in_=pos_ps[:])


            waiting = None
            to_multiply = []
            first = 0
            for count in LOADS:
                rows = load_passes(first, count)
                for g0 in range(0, count, STEP):
                    for g in range(g0, min(g0 + STEP, count)):
                        grouped = transpose_pass(rows, g)
                        if waiting is not None:
                            quantise_pass(*waiting)
                        pass_codes = new_codes()
                        waiting = (grouped, pass_codes)
                        to_multiply.append((first + g, pass_codes))
                    while to_multiply and to_multiply[0][0] <= first + g - LAG:
                        multiply_pass(*to_multiply.pop(0))
                first += count
            quantise_pass(*waiting)
            neg_sb = keep.tile([P, J_TILES, EMB_D], BF16)
            nc.sync.dma_start(out=neg_sb[:], in_=n_lfs.rearrange("(jt p) d -> p jt d", p=P))
            pos_sb = keep.tile([P, B_TILES, EMB_D], BF16)
            nc.sync.dma_start(out=pos_sb[:], in_=p_lfs.rearrange("(bt p) d -> p bt d", p=P))
            transpose_labels(neg_sb, pos_sb)
            for n, pass_codes in to_multiply:
                multiply_pass(n, pass_codes)

            hid_sb = [keep.tile([P, HID_D], F32, name="hid_sb%d" % bt) for bt in range(B_TILES)]
            nc.scalar.copy(out=hid_sb[0][:], in_=acc[0][:])
            nc.vector.tensor_copy(out=hid_sb[1][:], in_=acc[1][:])

            def add_bias(first_t, out_tile, bank, bias_col):
                for s in range(2):
                    t = first_t + s
                    bias = bias_cols[:, bias_col + t : bias_col + t + 1]
                    if first_t == 0:
                        nc.scalar.activation(
                            out=out_tile[:, t, :], in_=bank[:, s, :], func=ACT.Identity, bias=bias
                        )
                    else:
                        nc.vector.tensor_scalar(
                            out=out_tile[:, t, :], in0=bank[:, s, :],
                            scalar1=bias, scalar2=None, op0=ALU.add,
                        )

            hid_bf = keep.tile([P, H_TILES, B], BF16)
            for first_t in range(0, H_TILES, 2):
                hid_ps = bank_psum.tile([P, 2, B], F32, tag="bank")
                for s in range(2):
                    h_cols = slice((first_t + s) * P, (first_t + s + 1) * P)
                    for bt in range(B_TILES):
                        nc.tensor.transpose(
                            out=hid_ps[:, s, bt * P : (bt + 1) * P],
                            in_=hid_sb[bt][:, h_cols],
                            identity=ident_f32[:],
                        )
                add_bias(first_t, hid_bf, hid_ps, 0)
            hid_grouped = keep.tile([P, B, QUAD], BF16, align_bytes=64)
            nc.vector.tensor_copy(out=hid_grouped[:], in_=hid_bf[:].rearrange("p t b -> p b t"))
            hid_codes = keep.tile([P, B], U32, align_bytes=64)
            hid_scales = keep.tile([P, B], U8, align_bytes=64)
            nc.vector.quantize_mx(
                out=hid_codes[:].bitcast(FP8X4),
                scales=hid_scales[:],
                in_=hid_grouped[:].rearrange("p b t -> p (b t)"),
            )

            emb_banks = []
            for first_dt in range(0, D_TILES, 2):
                emb_ps = acc_psum.tile([P, 2, B], F32, name="acc%d" % (first_dt // 2))
                for s in range(2):
                    d_cols = slice((first_dt + s) * P, (first_dt + s + 1) * P)
                    nc.tensor.matmul_mx(
                        out=emb_ps[:, s, :],
                        lhsT=we_codes[:, d_cols].bitcast(FP8X4),
                        lhsT_scale=we_scales[:, d_cols],
                        rhs=hid_codes[:].bitcast(FP8X4),
                        rhs_scale=hid_scales[:],
                        start=True,
                        stop=True,
                    )
                add_bias(first_dt, high, emb_ps, H_TILES)
                emb_banks.append(emb_ps)
            nc.scalar.copy(out=high_f32[:, 0:2, :], in_=high[:, 0:2, :])
            nc.vector.tensor_copy(out=high_f32[:, 2:4, :], in_=high[:, 2:4, :])
            for dt in (2, 3, 0, 1):
                nc.vector.scalar_tensor_tensor(
                    out=parts[:, 1, dt, :],
                    in0=emb_banks[dt // 2][:, dt % 2, :],
                    scalar=bias_cols[:, H_TILES + dt : H_TILES + dt + 1],
                    in1=high_f32[:, dt, :],
                    op0=ALU.add,
                    op1=ALU.subtract,
                )
            for dt in range(D_TILES):
                nc.scalar.activation(
                    out=emb_t[:, dt, :],
                    in_=emb_banks[dt // 2][:, dt % 2, :],
                    func=ACT.Identity,
                    bias=bias_cols[:, H_TILES + dt : H_TILES + dt + 1],
                )

        with (
            tc.tile_pool(name="row_maxima", bufs=2 * LEAD + 2) as row_pool,
            tc.tile_pool(name="col_maxima", bufs=2 * LEAD + 2) as col_pool,
            tc.tile_pool(name="scratch", bufs=2) as scratch,
            tc.psum_pool(name="col_psum", bufs=1) as col_psum,
            tc.psum_pool(name="row_psum", bufs=2) as row_psum,
            tc.psum_pool(name="turn_psum", bufs=PSUM_BANKS - 3) as turn_psum,
        ):

            def transpose_four(source, cols):
                bank = turn_psum.tile([P, PER_BANK * P], F32, tag="bank")
                for t in range(PER_BANK):
                    nc.tensor.transpose(
                        out=bank[:, t * P : (t + 1) * P],
                        in_=source[:, t, cols],
                        identity=ident_f32[:],
                    )
                return bank

            def scalar_sum_of_squares(values, sum_col):
                squares = scratch.tile([P, EMB_D], F32, tag="squares")
                nc.scalar.activation(out=squares[:], in_=values, func=ACT.Square, accum_out=sum_col)

            row_sums = keep.tile([P, J_TILES, B], F32)
            square_sums = keep.tile([P, 2, B], F32)
            emb_squares = keep.tile([P, B_TILES], F32)
            pos_sums = keep.tile([P, B_TILES], F32)
            stats = keep.tile([P, len(VECTOR_ROWS), 2, STATS], F32)
            totals = keep.tile([P, B_TILES, N_NEG], F32)
            col_bank = col_psum.tile([P, B_TILES, PROD], F32, name="col_bank")

            def sum_own_squares():
                for jt in range(PROD_J_TILES):
                    scalar_sum_of_squares(neg_sb[:, jt, :], neg_squares[:, jt : jt + 1])
                for bt in range(B_TILES):
                    scalar_sum_of_squares(
                        transpose_four(emb_t, slice(bt * P, (bt + 1) * P))[:], emb_squares[:, bt : bt + 1]
                    )

            def positives():
                pos_clipped = keep.tile([P, D_TILES, B], F32)
                nc.vector.tensor_tensor(out=pos_clipped[:], in0=pos_t[:], in1=emb_t[:], op=ALU.subtract)
                nc.vector.tensor_scalar_max(out=pos_clipped[:], in0=pos_clipped[:], scalar1=0.0)
                for bt in range(B_TILES):
                    scalar_sum_of_squares(
                        transpose_four(pos_clipped, slice(bt * P, (bt + 1) * P))[:],
                        pos_sums[:, bt : bt + 1],
                    )

            def against(op, pool, source, scalars, index):
                result = pool.tile([P, D_TILES, source.shape[2]], BF16, tag="result")
                for dt in range(D_TILES):
                    nc.vector.tensor_scalar(
                        out=result[:, dt, :],
                        in0=source[:, dt, :],
                        scalar1=scalars[:, dt, index : index + 1],
                        scalar2=None,
                        op0=op,
                    )
                return result

            def turn(maxima, bank):
                for dt in range(D_TILES):
                    nc.tensor.transpose(
                        out=bank[:, dt * P : (dt + 1) * P],
                        in_=maxima[:, dt, PROD:].bitcast(F32),
                        identity=ident_f32[:],
                    )

            def four_products(out_cols, values, cols, weights):
                for dt in range(D_TILES):
                    nc.tensor.matmul(
                        out=out_cols,
                        lhsT=values[:, dt, cols],
                        rhs=weights(dt),
                        start=(dt == 0),
                        stop=(dt == D_TILES - 1),
                    )

            def row_groups(i, maxima, bank):
                return [
                    (
                        bank[:, jt, i % BANK_ROWS, :],
                        maxima,
                        slice(jt * P, (jt + 1) * P),
                        lambda dt: parts[:, :, dt, i],
                    )
                    for jt in range(J_TILES)
                ]

            def column_groups(j, minima):
                return [
                    (
                        col_bank[:, bt, j : j + 1],
                        minima,
                        slice(bt * P, (bt + 1) * P),
                        lambda dt: neg_bf[:, dt, j : j + 1],
                    )
                    for bt in range(B_TILES)
                ]

            def wide_pass(columns):
                bank = turn_psum.tile([P, PER_BANK * P], F32, tag="bank")
                nc.tensor.matmul_mx(
                    out=bank[:, 0:columns],
                    lhsT=we_codes[:, 0:P].bitcast(FP8X4),
                    lhsT_scale=we_scales[:, 0:P],
                    rhs=we_codes[:, 0:columns].bitcast(FP8X4),
                    rhs_scale=we_scales[:, 0:columns],
                    start=True,
                    stop=True,
                )
                return bank

            def sum_squares(i, bank):
                values = bank[:].bitcast(BF16).rearrange("p (d e) -> p e d", e=2)
                for e in range(2):
                    if i in VECTOR_ROWS:
                        nc.vector.bn_stats(
                            out=stats[:, VECTOR_ROWS.index(i), e, :], in_=values[:, e, :]
                        )
                    else:
                        scalar_sum_of_squares(values[:, e, :], square_sums[:, e, i : i + 1])

            def add_row_products(first_row, bank):
                i_cols = slice(first_row, first_row + BANK_ROWS)
                nc.vector.tensor_reduce(
                    out=row_sums[:, :, i_cols], in_=bank[:], axis=mybir.AxisListType.X, op=ALU.add
                )
                for jt in range(PROD_J_TILES):
                    nc.vector.scalar_tensor_tensor(
                        out=row_sums[:, jt, i_cols],
                        in0=row_sums[:, jt, i_cols],
                        scalar=neg_squares[:, jt : jt + 1],
                        in1=bank[:, jt, :, 1],
                        op0=ALU.subtract,
                        op1=ALU.add,
                    )

            def sums_from_stats(bt):
                count = len(VECTOR_ROWS) // B_TILES
                halves = stats[:, bt * count : (bt + 1) * count].rearrange(
                    "p i e (h k) -> p i e h k", k=STATS // 2
                )
                mean_squares = scratch.tile([P, count, 2, 2], F32, tag="mean_squares")
                nc.vector.tensor_tensor(
                    out=mean_squares[:], in0=halves[:, :, :, :, 1], in1=halves[:, :, :, :, 1], op=ALU.mult
                )
                half_sums = scratch.tile([P, count, 2, 2], F32, tag="half_sums")
                nc.vector.scalar_tensor_tensor(
                    out=half_sums[:],
                    in0=mean_squares[:],
                    scalar=float(EMB_D // 2),
                    in1=halves[:, :, :, :, 2],
                    op0=ALU.mult,
                    op1=ALU.add,
                )
                first = VECTOR_ROWS[bt * count]
                for e in range(2):
                    nc.vector.tensor_tensor(
                        out=square_sums[:, e, first : first + count * VECTOR_PERIOD : VECTOR_PERIOD],
                        in0=half_sums[:, :, e, 0],
                        in1=half_sums[:, :, e, 1],
                        op=ALU.add,
                    )

            roots = keep.tile([P, B_TILES, 1 + N_NEG], F32)
            scores = keep.tile([P, B_TILES, 1 + N_NEG], F32)

            def take_root(bt, first, end):
                half = totals[:, bt, first:end]
                nc.vector.tensor_scalar_max(out=half, in0=half, scalar1=0.0)
                nc.scalar.activation(out=roots[:, bt, 1 + first : 1 + end], in_=half, func=ACT.Sqrt)
                nc.vector.tensor_scalar_mul(
                    out=scores[:, bt, 1 + first : 1 + end],
                    in0=roots[:, bt, 1 + first : 1 + end],
                    scalar1=-1.0,
                )

            def finish_squares(bt):
                i_cols = slice(bt * P, (bt + 1) * P)
                squares_ps = turn_psum.tile([P, PER_BANK * P], F32, tag="bank")
                for e in range(2):
                    nc.tensor.transpose(
                        out=squares_ps[:, e * P : (e + 1) * P],
                        in_=square_sums[:, e, i_cols],
                        identity=ident_f32[:],
                    )
                nc.scalar.activation(
                    out=totals[:, bt, PROD:].rearrange("p (w e) -> p w e", e=2),
                    in_=squares_ps[:, 0:SQ].rearrange("p (e w) -> p w e", e=2),
                    func=ACT.Identity,
                    bias=emb_squares[:, bt : bt + 1],
                )
                rows_ps = transpose_four(row_sums, i_cols)
                nc.scalar.activation(
                    out=totals[:, bt, 0:PROD], in_=rows_ps[:, 0:PROD], func=ACT.Identity,
                    scale=-1.0, bias=emb_squares[:, bt : bt + 1],
                )
                nc.vector.scalar_tensor_tensor(
                    out=totals[:, bt, PROD:], in0=rows_ps[:, PROD:], scalar=-2.0,
                    in1=totals[:, bt, PROD:], op0=ALU.mult, op1=ALU.add,
                )
                nc.scalar.activation(out=roots[:, bt, 0:1], in_=pos_sums[:, bt : bt + 1], func=ACT.Sqrt)
                nc.vector.tensor_scalar_mul(out=scores[:, bt, 0:1], in0=roots[:, bt, 0:1], scalar1=-1.0)
                take_root(bt, PROD, N_NEG)

            def finish_products(bt):
                nc.vector.scalar_tensor_tensor(
                    out=totals[:, bt, 0:PROD], in0=col_bank[:, bt, :], scalar=-1.0,
                    in1=totals[:, bt, 0:PROD], op0=ALU.mult, op1=ALU.add,
                )
                take_root(bt, 0, PROD)
                nc.sync.dma_start(out=out[bt * P : (bt + 1) * P, :], in_=scores[:, bt, :])

            for columns in WIDE + WIDE:
                wide_pass(columns)
            made = []
            row_bank = None
            full_banks = []
            for step in range(0, B + LEAD, RUN):
                for i in range(step, min(step + RUN, B)):
                    maxima = against(ALU.max, row_pool, neg_bf, high_f32, i)
                    minima = against(ALU.min, col_pool, high, neg_t, i)
                    made.append((maxima, minima))
                if full_banks:
                    add_row_products(*full_banks.pop())
                if step >= LEAD:
                    rows = range(step - LEAD, step - LEAD + RUN)
                    banks = [wide_pass(columns) for columns in WIDE]
                    for i, bank in zip(rows, banks):
                        turn(made[i][0], bank)
                    groups = []
                    for i in rows:
                        if i % BANK_ROWS == 0:
                            row_bank = row_psum.tile([P, J_TILES, BANK_ROWS, 2], F32, tag="row_bank")
                        groups += row_groups(i, made[i][0], row_bank)
                        groups += column_groups(i, made[i][1])
                        if i % BANK_ROWS == BANK_ROWS - 1:
                            full_banks.append((i + 1 - BANK_ROWS, row_bank))
                    for group in groups:
                        four_products(*group)
                    for i, bank in zip(rows, banks):
                        sum_squares(i, bank)
                if step == 8:
                    sum_own_squares()
                elif step == 16:
                    positives()
                elif step == P + 10:
                    sums_from_stats(0)
                    finish_squares(0)
                elif step == B - 4:
                    sums_from_stats(1)
            add_row_products(*full_banks.pop())
            finish_products(0)
            finish_squares(1)
            finish_products(1)
